import numpy as np
import ml_dtypes


def mxq(x, axis, fmt="e4m3"):
    dtype, down = {"e4m3": (ml_dtypes.float8_e4m3fn, 7), "e5m2": (ml_dtypes.float8_e5m2, 14)}[fmt]
    v = np.moveaxis(np.asarray(x, np.float32).astype(ml_dtypes.bfloat16).astype(np.float64), axis, -1)
    blocks = v.reshape(v.shape[:-1] + (-1, 32))
    amax = np.abs(blocks).max(-1, keepdims=True)
    byte = np.maximum(np.where(amax > 0, np.frexp(amax)[1] - 1 + 127, 0) - down, 1)
    scale = np.exp2(byte - 127.0)
    codes = (blocks / scale).astype(np.float32).astype(dtype).astype(np.float64)
    return np.moveaxis((codes * scale).reshape(v.shape), -1, axis)


WIDE = False


def mx_kscale(k):
    if not WIDE:
        return np.ones(k)
    levels = np.array([10, -10, 5, -5, 0])
    a = np.random.permutation(np.resize(levels, k // 512 * 4)).reshape(k // 512, 4)
    idx = np.arange(k)
    return np.exp2(a[idx // 512, idx % 128 // 32])


BF16 = ml_dtypes.bfloat16


def bf(x):
    return np.asarray(x, np.float32).astype(BF16)


def f64(x):
    return np.asarray(x).astype(np.float64)


E2M1 = np.array([0.0, 0.5, 1.0, 1.5, 2.0, 3.0, 4.0, 6.0, -0.0, -0.5, -1.0, -1.5, -2.0, -3.0, -4.0, -6.0])


def pack_weight(w, fmt):
    k, n = w.shape
    w = f64(bf(w)).reshape(k // 32, 32, n)
    amax = np.abs(w).max(1)
    if fmt == "e4m3":
        byte = np.frexp(amax)[1] - 1 + 127 - 7
    else:
        mant, ex = np.frexp(amax / 6.0)
        byte = np.where(mant > 0.5, ex, ex - 1) + 127
    byte = np.clip(np.where(amax > 0, byte, 1), 1, 254)
    scaled = (w * np.exp2(127.0 - byte)[:, None, :]).reshape(k, n).astype(np.float32)
    by_word = np.ascontiguousarray(scaled.reshape(k // 512, 128, 4, n).transpose(0, 1, 3, 2))
    if fmt == "e4m3":
        words = by_word.astype(ml_dtypes.float8_e4m3fn).view(np.uint8)
    else:
        c = by_word.astype(ml_dtypes.float4_e2m1fn).view(np.uint8) & 0xF
        words = c[..., 0::2] | (c[..., 1::2] << 4)
    return np.ascontiguousarray(words), np.ascontiguousarray(byte.astype(np.uint8).reshape(k // 512, 16, n))


def unpack_weight(words, scales, fmt):
    g, p, n, _ = words.shape
    if fmt == "e4m3":
        vals = np.ascontiguousarray(words).view(ml_dtypes.float8_e4m3fn).astype(np.float64)
    else:
        nib = np.empty((g, p, n, 4), np.uint8)
        nib[..., 0::2] = words & 0xF
        nib[..., 1::2] = words >> 4
        vals = E2M1[nib]
    vals = vals * np.repeat(np.exp2(scales.astype(np.float64) - 127.0), 8, axis=1)[..., None]
    return vals.transpose(0, 1, 3, 2).reshape(g * 512, n)


B, GH, GW, F_IN, F_OUT = 2, 64, 64, 512, 512
FMT = "e4m3"


def setup_inputs():
    s = mx_kscale(F_IN)
    X = bf(np.random.standard_normal((B, GH * GW, F_IN)) * s)
    words, scales = pack_weight(np.random.standard_normal((F_IN, F_OUT)) * 0.5 / np.sqrt(F_IN) / s[:, None], FMT)
    b = bf(np.random.standard_normal(F_OUT) * 0.3)
    return {"X": X,
            "W_gcn_words": words,
            "W_gcn_scales": scales,
            "b": b,
            "H": GH, "Wd": GW}


def _neighbor_sum(Xg):
    p = np.pad(Xg, ((0, 0), (1, 1), (1, 1), (0, 0)))
    return (p[:, :-2, 1:-1] + p[:, 2:, 1:-1]
            + p[:, 1:-1, :-2] + p[:, 1:-1, 2:])


def reference(X, W_gcn_words, W_gcn_scales, b, H, Wd):
    X = f64(X)
    Bn, N, F = X.shape
    Xg = X.reshape(Bn, H, Wd, F)
    AX = _neighbor_sum(Xg).reshape(Bn, N, F)
    return (mxq(AX, 2, "e4m3") @ unpack_weight(W_gcn_words, W_gcn_scales, FMT)) + f64(b)

@@ -1,0 +1,179 @@
+from contextlib import ExitStack
+
+import concourse.mybir as mybir
+from concourse.masks import make_identity
+
+BF16 = mybir.dt.bfloat16
+F32 = mybir.dt.float32
+I32 = mybir.dt.int32
+U8 = mybir.dt.uint8
+U32 = mybir.dt.uint32
+FP8X4 = mybir.dt.float8_e4m3fn_x4
+ADD = mybir.AluOpType.add
+
+P = 128
+PACK = 4
+BATCH, GRID, F_IN, F_OUT = 2, 64, 512, 512
+PITCH = GRID + 1
+BAND = 8
+BANDS = BATCH * GRID // BAND
+TILES = BAND * GRID // P
+BANK_ROWS = 4
+BANK_TILES = BANK_ROWS * GRID // P
+WORDS = F_IN // 2
+LOADS_AHEAD = 4
+
+FLOPS = 2 * BATCH * GRID * GRID * F_IN * F_OUT
+
+
+def tile_graphconvlayer_kernel(tc, X, W_gcn_words, W_gcn_scales, b, H, Wd, out):
+    nc = tc.nc
+    assert (H, Wd) == (GRID, GRID)
+
+    with ExitStack() as ctx:
+        const = ctx.enter_context(tc.tile_pool(name="const", bufs=1))
+        loads = ctx.enter_context(tc.tile_pool(name="loads", bufs=LOADS_AHEAD))
+        work = ctx.enter_context(tc.tile_pool(name="work", bufs=3))
+        psum_t = ctx.enter_context(tc.psum_pool(name="psum_t", bufs=4))
+        psum_o = ctx.enter_context(tc.psum_pool(name="psum_o", bufs=4))
+
+        x_tiles, xT_tiles, ax_tiles, acc_tiles = {}, {}, {}, {}
+
+        def place(g):
+            return g * BAND // GRID, g * BAND % GRID
+
+        def load(g):
+            bi, i0 = place(g)
+            x_sb = loads.tile([P, TILES, F_IN], BF16, name="x_sb")
+            nc.sync.dma_start(
+                out=x_sb[:],
+                in_=X[bi, i0 * GRID : (i0 + BAND) * GRID, :].rearrange("(q p) f -> p q f", p=P),
+            )
+            x_tiles[g] = x_sb
+
+        for g in range(LOADS_AHEAD):
+            load(g)
+        ident = const.tile([P, P], F32, name="ident")
+        make_identity(nc, ident[:])
+
+        w_codes = const.tile([P, F_OUT * PACK], U8, name="w_codes", align_bytes=64)
+        nc.sync.dma_start(
+            out=w_codes[:].bitcast(I32),
+            in_=W_gcn_words[0].rearrange("p n t -> p (n t)").bitcast(I32),
+        )
+        w_scales = const.tile([P, F_OUT], U8, name="w_scales", align_bytes=64)
+        nc.vector.memset(w_scales[:].bitcast(I32), 0)
+        for quad in range(4):
+            nc.sync.dma_start(
+                out=w_scales[32 * quad : 32 * quad + 4, :].bitcast(I32),
+                in_=W_gcn_scales[0, 4 * quad : 4 * quad + 4, :].bitcast(I32),
+            )
+
+        bias_bf = const.tile([P, F_OUT], BF16, name="bias_bf")
+        nc.scalar.dma_start(out=bias_bf[:], in_=b.partition_broadcast(P))
+        bias = const.tile([P, F_OUT], F32, name="bias")
+        nc.vector.tensor_copy(out=bias[:], in_=bias_bf[:])
+
+        xt = const.tile([P, PITCH, PITCH, PACK], BF16, name="xt")
+        xt_words = xt[:].bitcast(F32)
+        pair_t = const.tile([P, PITCH, PITCH, PACK], F32, name="pair_t")
+        zeros = const.tile([P, PITCH, 2], F32, name="zeros")
+        nc.vector.memset(zeros[:], 0.0)
+        nc.scalar.copy(out=xt_words[:, 0, :, :], in_=zeros[:])
+        nc.scalar.copy(out=xt_words[:, :, 0, :], in_=zeros[:])
+
+        def transpose(g):
+            i0 = place(g)[1]
+            x_words = x_tiles[g][:].bitcast(F32)
+            xT_tiles[g] = []
+            for h in range(BAND // BANK_ROWS):
+                row = i0 + h * BANK_ROWS
+                xT = psum_t.tile([P, 2, BANK_ROWS * GRID], F32, name="xT")
+                for q in range(BANK_TILES):
+                    for u in range(2):
+                        nc.tensor.transpose(
+                            out=xT[:, u, q * P : (q + 1) * P],
+                            in_=x_words[:, h * BANK_TILES + q, u:WORDS:2],
+                            identity=ident[:],
+                        )
+                nc.scalar.copy(
+                    out=xt_words[:, row + 1 : row + 1 + BANK_ROWS, 1:PITCH, :],
+                    in_=xT[:].rearrange("p u (r c) -> p r c u", r=BANK_ROWS),
+                )
+                xT_tiles[g].append(xT)
+
+        def first_add(g):
+            i0 = place(g)[1]
+            for h, xT in enumerate(xT_tiles[g]):
+                rows = slice(i0 + h * BANK_ROWS, i0 + (h + 1) * BANK_ROWS)
+                nc.vector.tensor_tensor(
+                    out=pair_t[:, rows, 0:GRID, :].rearrange("p r c (u e) -> p r c u e", u=2),
+                    in0=xT[:].bitcast(BF16).rearrange("p u (r c e) -> p r c u e", r=BANK_ROWS, e=2),
+                    in1=xt[:, rows, 0:GRID, :].rearrange("p r c (u e) -> p r c u e", u=2),
+                    op=ADD,
+                )
+            nc.vector.tensor_copy(
+                out=pair_t[:, i0 : i0 + BAND, GRID, :], in_=xt[:, i0 : i0 + BAND, GRID, :]
+            )
+            if i0 + BAND == GRID:
+                nc.vector.tensor_copy(out=pair_t[:, GRID, :, :], in_=xt[:, GRID, :, :])
+
+        def second_add(g):
+            i0 = place(g)[1]
+            ax = work.tile([P, BAND, GRID, PACK], BF16, name="ax", align_bytes=64)
+            nc.gpsimd.tensor_tensor(
+                out=ax[:],
+                in0=pair_t[:, i0 : i0 + BAND, 1:PITCH, :],
+                in1=pair_t[:, i0 + 1 : i0 + 1 + BAND, 0:GRID, :],
+                op=ADD,
+            )
+            ax_tiles[g] = ax
+
+        def multiply(g):
+            ax = ax_tiles[g]
+            codes = work.tile([P, BAND * GRID], U32, name="codes", align_bytes=64)
+            scales = work.tile([P, BAND * GRID], U8, name="scales", align_bytes=64)
+            nc.vector.quantize_mx(
+                out=codes[:].bitcast(FP8X4),
+                scales=scales[:],
+                in_=ax[:].rearrange("p r c t -> p (r c t)"),
+            )
+            acc_tiles[g] = []
+            for q in range(TILES):
+                nodes = slice(q * P, (q + 1) * P)
+                acc = psum_o.tile([P, F_OUT], F32, name="acc")
+                nc.tensor.matmul_mx(
+                    out=acc[:],
+                    lhsT=codes[:, nodes].bitcast(FP8X4),
+                    lhsT_scale=scales[:, nodes],
+                    rhs=w_codes[:].bitcast(FP8X4),
+                    rhs_scale=w_scales[:],
+                    start=True,
+                    stop=True,
+                )
+                acc_tiles[g].append(acc)
+
+        def finish(g):
+            bi, i0 = place(g)
+            o_sb = work.tile([P, TILES, F_OUT], F32, name="o_sb")
+            for q, acc in enumerate(acc_tiles[g]):
+                nc.vector.tensor_tensor(out=o_sb[:, q, :], in0=acc[:], in1=bias[:], op=ADD)
+            nc.scalar.dma_start(
+                out=out[bi, i0 * GRID : (i0 + BAND) * GRID, :].rearrange("(q p) f -> p q f", p=P),
+                in_=o_sb[:],
+            )
+
+        transpose(0)
+        for step in range(BANDS + 3):
+            if step + LOADS_AHEAD < BANDS:
+                load(step + LOADS_AHEAD)
+            if 0 <= step - 3:
+                multiply(step - 3)
+            if step < BANDS:
+                first_add(step)
+            if step + 1 < BANDS:
+                transpose(step + 1)
+            if 0 <= step - 1 < BANDS:
+                second_add(step - 1)
+            if 0 <= step - 3:
+                finish(step - 3)

@@ -108,8 +108,8 @@ def tile_graphconvlayer_kernel(tc, X, W_gcn_words, W_gcn_scales, b, H, Wd, out):
                 rows = slice(i0 + h * BANK_ROWS, i0 + (h + 1) * BANK_ROWS)
                 nc.vector.tensor_tensor(
                     out=pair_t[:, rows, 0:GRID, :].rearrange("p r c (u e) -> p r c u e", u=2),
-                    in0=xT[:].bitcast(BF16).rearrange("p u (r c e) -> p r c u e", r=BANK_ROWS, e=2),
-                    in1=xt[:, rows, 0:GRID, :].rearrange("p r c (u e) -> p r c u e", u=2),
+                    in0=xt[:, rows, 0:GRID, :].rearrange("p r c (u e) -> p r c u e", u=2),
+                    in1=xT[:].bitcast(BF16).rearrange("p u (r c e) -> p r c u e", r=BANK_ROWS, e=2),
                     op=ADD,
                 )
             nc.vector.tensor_copy(
@@ -157,7 +157,7 @@ def tile_graphconvlayer_kernel(tc, X, W_gcn_words, W_gcn_scales, b, H, Wd, out):
             bi, i0 = place(g)
             o_sb = work.tile([P, TILES, F_OUT], F32, name="o_sb")
             for q, acc in enumerate(acc_tiles[g]):
-                nc.vector.tensor_tensor(out=o_sb[:, q, :], in0=acc[:], in1=bias[:], op=ADD)
+                nc.vector.tensor_tensor(out=o_sb[:, q, :], in0=bias[:], in1=acc[:], op=ADD)
             nc.scalar.dma_start(
                 out=out[bi, i0 * GRID : (i0 + BAND) * GRID, :].rearrange("(q p) f -> p q f", p=P),
                 in_=o_sb[:],

@@ -10,18 +10,23 @@ U8 = mybir.dt.uint8
 U32 = mybir.dt.uint32
 FP8X4 = mybir.dt.float8_e4m3fn_x4
 ADD = mybir.AluOpType.add
+IDENTITY = mybir.ActivationFunctionType.Identity
 
 P = 128
 PACK = 4
 BATCH, GRID, F_IN, F_OUT = 2, 64, 512, 512
 PITCH = GRID + 1
+DIAGONAL = PITCH + 1
 BAND = 8
+BAND_NODES = BAND * GRID
 BANDS = BATCH * GRID // BAND
-TILES = BAND * GRID // P
+TILES = BAND_NODES // P
+F_BLOCKS = F_OUT // P
 BANK_ROWS = 4
 BANK_TILES = BANK_ROWS * GRID // P
 WORDS = F_IN // 2
 LOADS_AHEAD = 4
+VECTOR_TILES = 1
 
 FLOPS = 2 * BATCH * GRID * GRID * F_IN * F_OUT
 
@@ -34,10 +39,10 @@ def tile_graphconvlayer_kernel(tc, X, W_gcn_words, W_gcn_scales, b, H, Wd, out):
         const = ctx.enter_context(tc.tile_pool(name="const", bufs=1))
         loads = ctx.enter_context(tc.tile_pool(name="loads", bufs=LOADS_AHEAD))
         work = ctx.enter_context(tc.tile_pool(name="work", bufs=3))
-        psum_t = ctx.enter_context(tc.psum_pool(name="psum_t", bufs=4))
-        psum_o = ctx.enter_context(tc.psum_pool(name="psum_o", bufs=4))
+        psum_x = ctx.enter_context(tc.psum_pool(name="psum_x", bufs=2))
+        psum_o = ctx.enter_context(tc.psum_pool(name="psum_o", bufs=3))
 
-        x_tiles, xT_tiles, ax_tiles, acc_tiles = {}, {}, {}, {}
+        x_tiles, ax_tiles, mx_tiles, outT_tiles = {}, {}, {}, {}
 
         def place(g):
             return g * BAND // GRID, g * BAND % GRID
@@ -56,7 +61,7 @@ def tile_graphconvlayer_kernel(tc, X, W_gcn_words, W_gcn_scales, b, H, Wd, out):
         ident = const.tile([P, P], F32, name="ident")
         make_identity(nc, ident[:])
 
-        w_codes = const.tile([P, F_OUT * PACK], U8, name="w_codes", align_bytes=64)
+        w_codes = const.tile([P, F_OUT], U32, name="w_codes", align_bytes=64)
         nc.sync.dma_start(
             out=w_codes[:].bitcast(I32),
             in_=W_gcn_words[0].rearrange("p n t -> p (n t)").bitcast(I32),
@@ -69,26 +74,31 @@ def tile_graphconvlayer_kernel(tc, X, W_gcn_words, W_gcn_scales, b, H, Wd, out):
                 in_=W_gcn_scales[0, 4 * quad : 4 * quad + 4, :].bitcast(I32),
             )
 
-        bias_bf = const.tile([P, F_OUT], BF16, name="bias_bf")
-        nc.scalar.dma_start(out=bias_bf[:], in_=b.partition_broadcast(P))
-        bias = const.tile([P, F_OUT], F32, name="bias")
-        nc.vector.tensor_copy(out=bias[:], in_=bias_bf[:])
+        b_rows = const.tile([P, P], BF16, name="b_rows")
+        nc.vector.memset(b_rows[:].bitcast(F32), 0.0)
+        nc.scalar.dma_start(out=b_rows[0:F_BLOCKS, :], in_=b.rearrange("(f p) -> f p", p=P))
+        b_rows_f32 = const.tile([P, P], F32, name="b_rows_f32")
+        nc.vector.tensor_copy(out=b_rows_f32[:], in_=b_rows[:])
+        b_ps = psum_o.tile([P, F_OUT], F32, name="back")
+        nc.tensor.transpose(out=b_ps[:, 0:P], in_=b_rows_f32[:], identity=ident[:])
+        bias_col = const.tile([P, F_BLOCKS], F32, name="bias_col")
+        nc.vector.tensor_copy(out=bias_col[:], in_=b_ps[:, 0:F_BLOCKS])
 
-        xt = const.tile([P, PITCH, PITCH, PACK], BF16, name="xt")
-        xt_words = xt[:].bitcast(F32)
-        pair_t = const.tile([P, PITCH, PITCH, PACK], F32, name="pair_t")
-        zeros = const.tile([P, PITCH, 2], F32, name="zeros")
+        xt = const.tile([P, (PITCH + 1) * PITCH, PACK], BF16, name="xt")
+        xt_grid = xt[:].bitcast(F32).rearrange("p (r c) u -> p r c u", c=PITCH)
+        pair_t = const.tile([P, PITCH * PITCH, PACK], F32, name="pair_t")
+        pair_grid = pair_t[:].rearrange("p (r c) t -> p r c t", c=PITCH)
+        zeros = const.tile([P, PITCH + 1, 2], F32, name="zeros")
         nc.vector.memset(zeros[:], 0.0)
-        nc.scalar.copy(out=xt_words[:, 0, :, :], in_=zeros[:])
-        nc.scalar.copy(out=xt_words[:, :, 0, :], in_=zeros[:])
+        nc.scalar.copy(out=xt_grid[:, 0, :, :], in_=zeros[:, 0:PITCH, :])
+        nc.scalar.copy(out=xt_grid[:, :, 0, :], in_=zeros[:])
 
         def transpose(g):
             i0 = place(g)[1]
             x_words = x_tiles[g][:].bitcast(F32)
-            xT_tiles[g] = []
             for h in range(BAND // BANK_ROWS):
                 row = i0 + h * BANK_ROWS
-                xT = psum_t.tile([P, 2, BANK_ROWS * GRID], F32, name="xT")
+                xT = psum_x.tile([P, 2, BANK_ROWS * GRID], F32, name="xT")
                 for q in range(BANK_TILES):
                     for u in range(2):
                         nc.tensor.transpose(
@@ -97,83 +107,98 @@ def tile_graphconvlayer_kernel(tc, X, W_gcn_words, W_gcn_scales, b, H, Wd, out):
                             identity=ident[:],
                         )
                 nc.scalar.copy(
-                    out=xt_words[:, row + 1 : row + 1 + BANK_ROWS, 1:PITCH, :],
+                    out=xt_grid[:, row + 1 : row + 1 + BANK_ROWS, 1:PITCH, :],
                     in_=xT[:].rearrange("p u (r c) -> p r c u", r=BANK_ROWS),
                 )
-                xT_tiles[g].append(xT)
 
         def first_add(g):
             i0 = place(g)[1]
-            for h, xT in enumerate(xT_tiles[g]):
-                rows = slice(i0 + h * BANK_ROWS, i0 + (h + 1) * BANK_ROWS)
-                nc.vector.tensor_tensor(
-                    out=pair_t[:, rows, 0:GRID, :].rearrange("p r c (u e) -> p r c u e", u=2),
-                    in0=xt[:, rows, 0:GRID, :].rearrange("p r c (u e) -> p r c u e", u=2),
-                    in1=xT[:].bitcast(BF16).rearrange("p u (r c e) -> p r c u e", r=BANK_ROWS, e=2),
-                    op=ADD,
-                )
-            nc.vector.tensor_copy(
-                out=pair_t[:, i0 : i0 + BAND, GRID, :], in_=xt[:, i0 : i0 + BAND, GRID, :]
+            first, last = i0 * PITCH, (i0 + BAND) * PITCH
+            nc.vector.tensor_tensor(
+                out=pair_t[:, first:last, :],
+                in0=xt[:, first:last, :],
+                in1=xt[:, first + DIAGONAL : last + DIAGONAL, :],
+                op=ADD,
             )
             if i0 + BAND == GRID:
-                nc.vector.tensor_copy(out=pair_t[:, GRID, :, :], in_=xt[:, GRID, :, :])
+                nc.vector.tensor_copy(out=pair_t[:, last:, :], in_=xt[:, last : last + PITCH, :])
 
         def second_add(g):
             i0 = place(g)[1]
             ax = work.tile([P, BAND, GRID, PACK], BF16, name="ax", align_bytes=64)
-            nc.gpsimd.tensor_tensor(
+            nc.vector.tensor_tensor(
                 out=ax[:],
-                in0=pair_t[:, i0 : i0 + BAND, 1:PITCH, :],
-                in1=pair_t[:, i0 + 1 : i0 + 1 + BAND, 0:GRID, :],
+                in0=pair_grid[:, i0 : i0 + BAND, 1:PITCH, :],
+                in1=pair_grid[:, i0 + 1 : i0 + 1 + BAND, 0:GRID, :],
                 op=ADD,
             )
             ax_tiles[g] = ax
 
-        def multiply(g):
-            ax = ax_tiles[g]
-            codes = work.tile([P, BAND * GRID], U32, name="codes", align_bytes=64)
-            scales = work.tile([P, BAND * GRID], U8, name="scales", align_bytes=64)
+        def quantise(g):
+            codes = work.tile([P, BAND_NODES], U32, name="codes", align_bytes=64)
+            scales = work.tile([P, BAND_NODES], U8, name="scales", align_bytes=64)
             nc.vector.quantize_mx(
                 out=codes[:].bitcast(FP8X4),
                 scales=scales[:],
-                in_=ax[:].rearrange("p r c t -> p (r c t)"),
+                in_=ax_tiles[g][:].rearrange("p r c t -> p (r c t)"),
             )
-            acc_tiles[g] = []
-            for q in range(TILES):
-                nodes = slice(q * P, (q + 1) * P)
-                acc = psum_o.tile([P, F_OUT], F32, name="acc")
+            mx_tiles[g] = (codes, scales)
+
+        def multiply(g):
+            codes, scales = mx_tiles[g]
+            outT = work.tile([P, F_BLOCKS, BAND_NODES], F32, name="outT")
+            for f in range(F_BLOCKS):
+                cols = slice(f * P, (f + 1) * P)
+                acc = psum_o.tile([P, BAND_NODES], F32, name="acc")
                 nc.tensor.matmul_mx(
                     out=acc[:],
-                    lhsT=codes[:, nodes].bitcast(FP8X4),
-                    lhsT_scale=scales[:, nodes],
-                    rhs=w_codes[:].bitcast(FP8X4),
-                    rhs_scale=w_scales[:],
+                    lhsT=w_codes[:, cols].bitcast(FP8X4),
+                    lhsT_scale=w_scales[:, cols],
+                    rhs=codes[:].bitcast(FP8X4),
+                    rhs_scale=scales[:],
                     start=True,
                     stop=True,
                 )
-                acc_tiles[g].append(acc)
+                nc.scalar.activation(
+                    out=outT[:, f, :], in_=acc[:], func=IDENTITY, bias=bias_col[:, f : f + 1], scale=1.0
+                )
+            outT_tiles[g] = outT
 
-        def finish(g):
+        def transpose_back(g):
             bi, i0 = place(g)
+            outT = outT_tiles[g]
             o_sb = work.tile([P, TILES, F_OUT], F32, name="o_sb")
-            for q, acc in enumerate(acc_tiles[g]):
-                nc.vector.tensor_tensor(out=o_sb[:, q, :], in0=bias[:], in1=acc[:], op=ADD)
-            nc.scalar.dma_start(
+            for q in range(TILES):
+                back = psum_o.tile([P, F_OUT], F32, name="back")
+                for f in range(F_BLOCKS):
+                    nc.tensor.transpose(
+                        out=back[:, f * P : (f + 1) * P],
+                        in_=outT[:, f, q * P : (q + 1) * P],
+                        identity=ident[:],
+                    )
+                if q < TILES - VECTOR_TILES:
+                    nc.scalar.copy(out=o_sb[:, q, :], in_=back[:])
+                else:
+                    nc.vector.tensor_copy(out=o_sb[:, q, :], in_=back[:])
+            nc.sync.dma_start(
                 out=out[bi, i0 * GRID : (i0 + BAND) * GRID, :].rearrange("(q p) f -> p q f", p=P),
                 in_=o_sb[:],
             )
 
+        ctx.enter_context(tc.manual_schedule())
         transpose(0)
         for step in range(BANDS + 3):
             if step + LOADS_AHEAD < BANDS:
                 load(step + LOADS_AHEAD)
-            if 0 <= step - 3:
-                multiply(step - 3)
-            if step < BANDS:
-                first_add(step)
             if step + 1 < BANDS:
                 transpose(step + 1)
+            if 0 <= step - 2 < BANDS:
+                quantise(step - 2)
+            if step < BANDS:
+                first_add(step)
             if 0 <= step - 1 < BANDS:
                 second_add(step - 1)
-            if 0 <= step - 3:
-                finish(step - 3)
+            if 0 <= step - 3 < BANDS:
+                transpose_back(step - 3)
+            if 0 <= step - 2 < BANDS:
+                multiply(step - 2)

@@ -26,7 +26,8 @@ BANK_ROWS = 4
 BANK_TILES = BANK_ROWS * GRID // P
 WORDS = F_IN // 2
 LOADS_AHEAD = 4
-VECTOR_TILES = 1
+XT_AHEAD = 6
+VECTOR_TILES = 0
 
 FLOPS = 2 * BATCH * GRID * GRID * F_IN * F_OUT
 
@@ -39,6 +40,7 @@ def tile_graphconvlayer_kernel(tc, X, W_gcn_words, W_gcn_scales, b, H, Wd, out):
         const = ctx.enter_context(tc.tile_pool(name="const", bufs=1))
         loads = ctx.enter_context(tc.tile_pool(name="loads", bufs=LOADS_AHEAD))
         work = ctx.enter_context(tc.tile_pool(name="work", bufs=3))
+        stores = ctx.enter_context(tc.tile_pool(name="stores", bufs=2 * TILES))
         psum_x = ctx.enter_context(tc.psum_pool(name="psum_x", bufs=2))
         psum_o = ctx.enter_context(tc.psum_pool(name="psum_o", bufs=3))
 
@@ -79,10 +81,12 @@ def tile_graphconvlayer_kernel(tc, X, W_gcn_words, W_gcn_scales, b, H, Wd, out):
         nc.scalar.dma_start(out=b_rows[0:F_BLOCKS, :], in_=b.rearrange("(f p) -> f p", p=P))
         b_rows_f32 = const.tile([P, P], F32, name="b_rows_f32")
         nc.vector.tensor_copy(out=b_rows_f32[:], in_=b_rows[:])
-        b_ps = psum_o.tile([P, F_OUT], F32, name="back")
-        nc.tensor.transpose(out=b_ps[:, 0:P], in_=b_rows_f32[:], identity=ident[:])
         bias_col = const.tile([P, F_BLOCKS], F32, name="bias_col")
-        nc.vector.tensor_copy(out=bias_col[:], in_=b_ps[:, 0:F_BLOCKS])
+
+        def transpose_bias():
+            b_ps = psum_o.tile([P, F_OUT], F32, name="back")
+            nc.tensor.transpose(out=b_ps[:, 0:P], in_=b_rows_f32[:], identity=ident[:])
+            nc.vector.tensor_copy(out=bias_col[:], in_=b_ps[:, 0:F_BLOCKS])
 
         xt = const.tile([P, (PITCH + 1) * PITCH, PACK], BF16, name="xt")
         xt_grid = xt[:].bitcast(F32).rearrange("p (r c) u -> p r c u", c=PITCH)
@@ -167,7 +171,6 @@ def tile_graphconvlayer_kernel(tc, X, W_gcn_words, W_gcn_scales, b, H, Wd, out):
         def transpose_back(g):
             bi, i0 = place(g)
             outT = outT_tiles[g]
-            o_sb = work.tile([P, TILES, F_OUT], F32, name="o_sb")
             for q in range(TILES):
                 back = psum_o.tile([P, F_OUT], F32, name="back")
                 for f in range(F_BLOCKS):
@@ -176,29 +179,33 @@ def tile_graphconvlayer_kernel(tc, X, W_gcn_words, W_gcn_scales, b, H, Wd, out):
                         in_=outT[:, f, q * P : (q + 1) * P],
                         identity=ident[:],
                     )
+                o_sb = stores.tile([P, F_OUT], F32, name="o_sb")
                 if q < TILES - VECTOR_TILES:
-                    nc.scalar.copy(out=o_sb[:, q, :], in_=back[:])
+                    nc.scalar.copy(out=o_sb[:], in_=back[:])
                 else:
-                    nc.vector.tensor_copy(out=o_sb[:, q, :], in_=back[:])
-            nc.sync.dma_start(
-                out=out[bi, i0 * GRID : (i0 + BAND) * GRID, :].rearrange("(q p) f -> p q f", p=P),
-                in_=o_sb[:],
-            )
+                    nc.vector.tensor_copy(out=o_sb[:], in_=back[:])
+                node = i0 * GRID + q * P
+                nc.sync.dma_start(out=out[bi, node : node + P, :], in_=o_sb[:])
 
         ctx.enter_context(tc.manual_schedule())
-        transpose(0)
-        for step in range(BANDS + 3):
-            if step + LOADS_AHEAD < BANDS:
-                load(step + LOADS_AHEAD)
-            if step + 1 < BANDS:
-                transpose(step + 1)
-            if 0 <= step - 2 < BANDS:
+
+        def fill_xt(g):
+            if g < BANDS:
+                transpose(g)
+            if g + LOADS_AHEAD < BANDS:
+                load(g + LOADS_AHEAD)
+
+        for g in range(XT_AHEAD):
+            fill_xt(g)
+        transpose_bias()
+        for step in range(BANDS + 2):
+            if 0 <= step - 2:
                 quantise(step - 2)
+                multiply(step - 2)
+            fill_xt(step + XT_AHEAD)
             if step < BANDS:
                 first_add(step)
             if 0 <= step - 1 < BANDS:
                 second_add(step - 1)
-            if 0 <= step - 3 < BANDS:
-                transpose_back(step - 3)
-            if 0 <= step - 2 < BANDS:
-                multiply(step - 2)
+            if 0 <= step - 2:
+                transpose_back(step - 2)

@@ -27,7 +27,7 @@ BANK_TILES = BANK_ROWS * GRID // P
 WORDS = F_IN // 2
 LOADS_AHEAD = 4
 XT_AHEAD = 6
-VECTOR_TILES = 0
+VECTOR_BANDS = 2
 
 FLOPS = 2 * BATCH * GRID * GRID * F_IN * F_OUT
 
@@ -180,7 +180,7 @@ def tile_graphconvlayer_kernel(tc, X, W_gcn_words, W_gcn_scales, b, H, Wd, out):
                         identity=ident[:],
                     )
                 o_sb = stores.tile([P, F_OUT], F32, name="o_sb")
-                if q < TILES - VECTOR_TILES:
+                if g < BANDS - VECTOR_BANDS:
                     nc.scalar.copy(out=o_sb[:], in_=back[:])
                 else:
                     nc.vector.tensor_copy(out=o_sb[:], in_=back[:])
@@ -195,17 +195,18 @@ def tile_graphconvlayer_kernel(tc, X, W_gcn_words, W_gcn_scales, b, H, Wd, out):
             if g + LOADS_AHEAD < BANDS:
                 load(g + LOADS_AHEAD)
 
-        for g in range(XT_AHEAD):
-            fill_xt(g)
+        fill_xt(0)
         transpose_bias()
-        for step in range(BANDS + 2):
-            if 0 <= step - 2:
-                quantise(step - 2)
-                multiply(step - 2)
-            fill_xt(step + XT_AHEAD)
+        for g in range(1, XT_AHEAD):
+            fill_xt(g)
+        for step in range(BANDS + 3):
             if step < BANDS:
                 first_add(step)
+            if 0 <= step - 2 < BANDS:
+                quantise(step - 2)
+                multiply(step - 2)
+            if 0 <= step - 3:
+                transpose_back(step - 3)
+            fill_xt(step + XT_AHEAD)
             if 0 <= step - 1 < BANDS:
                 second_add(step - 1)
-            if 0 <= step - 2:
-                transpose_back(step - 2)

@@ -26,8 +26,8 @@ BANK_ROWS = 4
 BANK_TILES = BANK_ROWS * GRID // P
 WORDS = F_IN // 2
 LOADS_AHEAD = 4
-XT_AHEAD = 6
-VECTOR_BANDS = 2
+XT_AHEAD = 10
+DIRECT_BANDS = 1
 
 FLOPS = 2 * BATCH * GRID * GRID * F_IN * F_OUT
 
@@ -41,8 +41,8 @@ def tile_graphconvlayer_kernel(tc, X, W_gcn_words, W_gcn_scales, b, H, Wd, out):
         loads = ctx.enter_context(tc.tile_pool(name="loads", bufs=LOADS_AHEAD))
         work = ctx.enter_context(tc.tile_pool(name="work", bufs=3))
         stores = ctx.enter_context(tc.tile_pool(name="stores", bufs=2 * TILES))
-        psum_x = ctx.enter_context(tc.psum_pool(name="psum_x", bufs=2))
-        psum_o = ctx.enter_context(tc.psum_pool(name="psum_o", bufs=3))
+        psum_mx = ctx.enter_context(tc.psum_pool(name="psum_mx", bufs=3))
+        psum_tr = ctx.enter_context(tc.psum_pool(name="psum_tr", bufs=5))
 
         x_tiles, ax_tiles, mx_tiles, outT_tiles = {}, {}, {}, {}
 
@@ -82,27 +82,34 @@ def tile_graphconvlayer_kernel(tc, X, W_gcn_words, W_gcn_scales, b, H, Wd, out):
         b_rows_f32 = const.tile([P, P], F32, name="b_rows_f32")
         nc.vector.tensor_copy(out=b_rows_f32[:], in_=b_rows[:])
         bias_col = const.tile([P, F_BLOCKS], F32, name="bias_col")
+        bias_row_bf = const.tile([P, F_OUT], BF16, name="bias_row_bf")
+        nc.scalar.dma_start(out=bias_row_bf[:], in_=b.partition_broadcast(P))
+        bias_row = const.tile([P, F_OUT], F32, name="bias_row")
+        nc.vector.tensor_copy(out=bias_row[:], in_=bias_row_bf[:])
 
         def transpose_bias():
-            b_ps = psum_o.tile([P, F_OUT], F32, name="back")
+            b_ps = psum_tr.tile([P, F_OUT], F32, name="b_ps", tag="tr")
             nc.tensor.transpose(out=b_ps[:, 0:P], in_=b_rows_f32[:], identity=ident[:])
             nc.vector.tensor_copy(out=bias_col[:], in_=b_ps[:, 0:F_BLOCKS])
 
-        xt = const.tile([P, (PITCH + 1) * PITCH, PACK], BF16, name="xt")
-        xt_grid = xt[:].bitcast(F32).rearrange("p (r c) u -> p r c u", c=PITCH)
+        xt = [
+            const.tile([P, (PITCH + 1) * PITCH, PACK], BF16, name="xt%d" % bi) for bi in range(BATCH)
+        ]
+        xt_grid = [t[:].bitcast(F32).rearrange("p (r c) u -> p r c u", c=PITCH) for t in xt]
         pair_t = const.tile([P, PITCH * PITCH, PACK], F32, name="pair_t")
         pair_grid = pair_t[:].rearrange("p (r c) t -> p r c t", c=PITCH)
         zeros = const.tile([P, PITCH + 1, 2], F32, name="zeros")
         nc.vector.memset(zeros[:], 0.0)
-        nc.scalar.copy(out=xt_grid[:, 0, :, :], in_=zeros[:, 0:PITCH, :])
-        nc.scalar.copy(out=xt_grid[:, :, 0, :], in_=zeros[:])
+        for grid in xt_grid:
+            nc.scalar.copy(out=grid[:, 0, :, :], in_=zeros[:, 0:PITCH, :])
+            nc.scalar.copy(out=grid[:, :, 0, :], in_=zeros[:])
 
         def transpose(g):
-            i0 = place(g)[1]
+            bi, i0 = place(g)
             x_words = x_tiles[g][:].bitcast(F32)
             for h in range(BAND // BANK_ROWS):
                 row = i0 + h * BANK_ROWS
-                xT = psum_x.tile([P, 2, BANK_ROWS * GRID], F32, name="xT")
+                xT = psum_tr.tile([P, 2, BANK_ROWS * GRID], F32, name="xT", tag="tr")
                 for q in range(BANK_TILES):
                     for u in range(2):
                         nc.tensor.transpose(
@@ -111,21 +118,21 @@ def tile_graphconvlayer_kernel(tc, X, W_gcn_words, W_gcn_scales, b, H, Wd, out):
                             identity=ident[:],
                         )
                 nc.scalar.copy(
-                    out=xt_grid[:, row + 1 : row + 1 + BANK_ROWS, 1:PITCH, :],
+                    out=xt_grid[bi][:, row + 1 : row + 1 + BANK_ROWS, 1:PITCH, :],
                     in_=xT[:].rearrange("p u (r c) -> p r c u", r=BANK_ROWS),
                 )
 
         def first_add(g):
-            i0 = place(g)[1]
+            bi, i0 = place(g)
             first, last = i0 * PITCH, (i0 + BAND) * PITCH
             nc.vector.tensor_tensor(
                 out=pair_t[:, first:last, :],
-                in0=xt[:, first:last, :],
-                in1=xt[:, first + DIAGONAL : last + DIAGONAL, :],
+                in0=xt[bi][:, first:last, :],
+                in1=xt[bi][:, first + DIAGONAL : last + DIAGONAL, :],
                 op=ADD,
             )
             if i0 + BAND == GRID:
-                nc.vector.tensor_copy(out=pair_t[:, last:, :], in_=xt[:, last : last + PITCH, :])
+                nc.vector.tensor_copy(out=pair_t[:, last:, :], in_=xt[bi][:, last : last + PITCH, :])
 
         def second_add(g):
             i0 = place(g)[1]
@@ -153,7 +160,7 @@ def tile_graphconvlayer_kernel(tc, X, W_gcn_words, W_gcn_scales, b, H, Wd, out):
             outT = work.tile([P, F_BLOCKS, BAND_NODES], F32, name="outT")
             for f in range(F_BLOCKS):
                 cols = slice(f * P, (f + 1) * P)
-                acc = psum_o.tile([P, BAND_NODES], F32, name="acc")
+                acc = psum_mx.tile([P, BAND_NODES], F32, name="acc")
                 nc.tensor.matmul_mx(
                     out=acc[:],
                     lhsT=w_codes[:, cols].bitcast(FP8X4),
@@ -172,7 +179,7 @@ def tile_graphconvlayer_kernel(tc, X, W_gcn_words, W_gcn_scales, b, H, Wd, out):
             bi, i0 = place(g)
             outT = outT_tiles[g]
             for q in range(TILES):
-                back = psum_o.tile([P, F_OUT], F32, name="back")
+                back = psum_tr.tile([P, F_OUT], F32, name="back", tag="tr")
                 for f in range(F_BLOCKS):
                     nc.tensor.transpose(
                         out=back[:, f * P : (f + 1) * P],
@@ -180,10 +187,27 @@ def tile_graphconvlayer_kernel(tc, X, W_gcn_words, W_gcn_scales, b, H, Wd, out):
                         identity=ident[:],
                     )
                 o_sb = stores.tile([P, F_OUT], F32, name="o_sb")
-                if g < BANDS - VECTOR_BANDS:
-                    nc.scalar.copy(out=o_sb[:], in_=back[:])
-                else:
-                    nc.vector.tensor_copy(out=o_sb[:], in_=back[:])
+                nc.scalar.copy(out=o_sb[:], in_=back[:])
+                node = i0 * GRID + q * P
+                nc.sync.dma_start(out=out[bi, node : node + P, :], in_=o_sb[:])
+
+        def multiply_direct(g):
+            bi, i0 = place(g)
+            codes, scales = mx_tiles[g]
+            for q in range(TILES):
+                nodes = slice(q * P, (q + 1) * P)
+                acc = psum_mx.tile([P, F_OUT], F32, name="acc")
+                nc.tensor.matmul_mx(
+                    out=acc[:],
+                    lhsT=codes[:, nodes].bitcast(FP8X4),
+                    lhsT_scale=scales[:, nodes],
+                    rhs=w_codes[:].bitcast(FP8X4),
+                    rhs_scale=w_scales[:],
+                    start=True,
+                    stop=True,
+                )
+                o_sb = stores.tile([P, F_OUT], F32, name="o_sb")
+                nc.vector.tensor_tensor(out=o_sb[:], in0=acc[:], in1=bias_row[:], op=ADD)
                 node = i0 * GRID + q * P
                 nc.sync.dma_start(out=out[bi, node : node + P, :], in_=o_sb[:])
 
@@ -199,13 +223,17 @@ def tile_graphconvlayer_kernel(tc, X, W_gcn_words, W_gcn_scales, b, H, Wd, out):
         transpose_bias()
         for g in range(1, XT_AHEAD):
             fill_xt(g)
-        for step in range(BANDS + 3):
+        turned = BANDS - DIRECT_BANDS
+        for step in range(BANDS + 2):
             if step < BANDS:
                 first_add(step)
             if 0 <= step - 2 < BANDS:
                 quantise(step - 2)
+            if 0 <= step - 2 < turned:
                 multiply(step - 2)
-            if 0 <= step - 3:
+            if turned <= step - 2 < BANDS:
+                multiply_direct(step - 2)
+            if 0 <= step - 3 < turned:
                 transpose_back(step - 3)
             fill_xt(step + XT_AHEAD)
             if 0 <= step - 1 < BANDS:

@@ -10,7 +10,10 @@ U8 = mybir.dt.uint8
 U32 = mybir.dt.uint32
 FP8X4 = mybir.dt.float8_e4m3fn_x4
 ADD = mybir.AluOpType.add
+NOT_EQUAL = mybir.AluOpType.not_equal
 IDENTITY = mybir.ActivationFunctionType.Identity
+
+MANUAL = True
 
 P = 128
 PACK = 4
@@ -19,14 +22,31 @@ PITCH = GRID + 1
 DIAGONAL = PITCH + 1
 BAND = 8
 BAND_NODES = BAND * GRID
-BANDS = BATCH * GRID // BAND
 TILES = BAND_NODES // P
 F_BLOCKS = F_OUT // P
 BANK_ROWS = 4
 BANK_TILES = BANK_ROWS * GRID // P
 WORDS = F_IN // 2
-LOADS_AHEAD = 4
-XT_AHEAD = 10
+
+ADD_ROWS = 40
+ADD_BANDS = ADD_ROWS // BAND
+BANDS = BATCH * ADD_BANDS
+ADD_TOP = (0, GRID + GRID - ADD_ROWS)
+XT_ROWS = ADD_ROWS + 3
+PAIR_ROWS = ADD_ROWS + 1
+STRIP = 6
+STRIP_TOP = ADD_ROWS
+STRIPS = (BATCH * GRID - BATCH * ADD_ROWS) // STRIP
+STRIP_NODES = STRIP * GRID
+STRIP_TILES = STRIP_NODES // P
+PATCH_ROWS, PATCH_COLS = STRIP + 2, 16
+WINDOW = PATCH_COLS - 3
+WINDOW_NODES = STRIP * WINDOW
+PATCHES = 5
+FAR = 1000
+
+BANDS_AHEAD = 5
+STRIPS_AHEAD = 3
 DIRECT_BANDS = 1
 
 FLOPS = 2 * BATCH * GRID * GRID * F_IN * F_OUT
@@ -35,31 +55,63 @@ FLOPS = 2 * BATCH * GRID * GRID * F_IN * F_OUT
 def tile_graphconvlayer_kernel(tc, X, W_gcn_words, W_gcn_scales, b, H, Wd, out):
     nc = tc.nc
     assert (H, Wd) == (GRID, GRID)
+    x_flat = X.rearrange("b n f -> (b n) f")
+    out_flat = out.rearrange("b n f -> (b n) f")
 
     with ExitStack() as ctx:
         const = ctx.enter_context(tc.tile_pool(name="const", bufs=1))
-        loads = ctx.enter_context(tc.tile_pool(name="loads", bufs=LOADS_AHEAD))
+        loads = ctx.enter_context(tc.tile_pool(name="loads", bufs=BANDS_AHEAD))
+        patches = ctx.enter_context(tc.tile_pool(name="patches", bufs=STRIPS_AHEAD * PATCHES))
         work = ctx.enter_context(tc.tile_pool(name="work", bufs=3))
-        stores = ctx.enter_context(tc.tile_pool(name="stores", bufs=2 * TILES))
-        psum_mx = ctx.enter_context(tc.psum_pool(name="psum_mx", bufs=3))
-        psum_tr = ctx.enter_context(tc.psum_pool(name="psum_tr", bufs=5))
+        waiting = ctx.enter_context(tc.tile_pool(name="waiting", bufs=STRIPS_AHEAD + 2))
+        stores_s = ctx.enter_context(tc.tile_pool(name="stores_s", bufs=6))
+        stores_v = ctx.enter_context(tc.tile_pool(name="stores_v", bufs=5))
+        to_scalar = ctx.enter_context(tc.psum_pool(name="to_scalar", bufs=5))
+        to_vector = ctx.enter_context(tc.psum_pool(name="to_vector", bufs=3))
 
         x_tiles, ax_tiles, mx_tiles, outT_tiles = {}, {}, {}, {}
+        patch_tiles, strip_ax, strip_mx = {}, {}, {}
 
         def place(g):
-            return g * BAND // GRID, g * BAND % GRID
+            bi, i0 = g // ADD_BANDS, g % ADD_BANDS * BAND
+            return bi, i0, ADD_TOP[bi] + i0
 
-        def load(g):
-            bi, i0 = place(g)
-            x_sb = loads.tile([P, TILES, F_IN], BF16, name="x_sb")
-            nc.sync.dma_start(
-                out=x_sb[:],
-                in_=X[bi, i0 * GRID : (i0 + BAND) * GRID, :].rearrange("(q p) f -> p q f", p=P),
-            )
-            x_tiles[g] = x_sb
+        def load_unit(kind, g):
+            if kind == "band":
+                row = place(g)[2]
+                x_sb = loads.tile([P, TILES, F_IN], BF16, name="x_sb")
+                nc.sync.dma_start(
+                    out=x_sb[:],
+                    in_=x_flat[row * GRID : (row + BAND) * GRID, :].rearrange("(q p) f -> p q f", p=P),
+                )
+            else:
+                row = ADD_ROWS if g == 0 else ADD_TOP[1] - 2
+                x_sb = loads.tile([P, 1, F_IN], BF16, name="x_edge")
+                nc.sync.dma_start(
+                    out=x_sb[:],
+                    in_=x_flat[row * GRID : (row + 2) * GRID, :].rearrange("(q p) f -> p q f", p=P),
+                )
+            x_tiles[(kind, g)] = x_sb
 
-        for g in range(LOADS_AHEAD):
-            load(g)
+        def window_col(h):
+            return min(h * WINDOW, GRID - WINDOW)
+
+        def load_strip(e):
+            row = STRIP_TOP + e * STRIP
+            for h in range(PATCHES):
+                first = (row - 1) * GRID + window_col(h) - 1
+                xk = patches.tile([P, F_IN], BF16, name="xk")
+                nc.sync.dma_start(
+                    out=xk[:],
+                    in_=x_flat[first : first + PATCH_ROWS * GRID, :].rearrange("(r c) f -> c r f", c=GRID)[
+                        0:PATCH_COLS, :, :
+                    ],
+                )
+                patch_tiles[(e, h)] = xk
+
+        for g in range(4):
+            load_unit("band", g)
+        load_strip(0)
         ident = const.tile([P, P], F32, name="ident")
         make_identity(nc, ident[:])
 
@@ -75,6 +127,9 @@ def tile_graphconvlayer_kernel(tc, X, W_gcn_words, W_gcn_scales, b, H, Wd, out):
                 out=w_scales[32 * quad : 32 * quad + 4, :].bitcast(I32),
                 in_=W_gcn_scales[0, 4 * quad : 4 * quad + 4, :].bitcast(I32),
             )
+        load_strip(1)
+        load_unit("band", 4)
+        load_strip(2)
 
         b_rows = const.tile([P, P], BF16, name="b_rows")
         nc.vector.memset(b_rows[:].bitcast(F32), 0.0)
@@ -88,51 +143,101 @@ def tile_graphconvlayer_kernel(tc, X, W_gcn_words, W_gcn_scales, b, H, Wd, out):
         nc.vector.tensor_copy(out=bias_row[:], in_=bias_row_bf[:])
 
         def transpose_bias():
-            b_ps = psum_tr.tile([P, F_OUT], F32, name="b_ps", tag="tr")
+            b_ps = to_vector.tile([P, F_OUT], F32, name="b_ps", tag="v")
             nc.tensor.transpose(out=b_ps[:, 0:P], in_=b_rows_f32[:], identity=ident[:])
             nc.vector.tensor_copy(out=bias_col[:], in_=b_ps[:, 0:F_BLOCKS])
 
-        xt = [
-            const.tile([P, (PITCH + 1) * PITCH, PACK], BF16, name="xt%d" % bi) for bi in range(BATCH)
-        ]
-        xt_grid = [t[:].bitcast(F32).rearrange("p (r c) u -> p r c u", c=PITCH) for t in xt]
-        pair_t = const.tile([P, PITCH * PITCH, PACK], F32, name="pair_t")
-        pair_grid = pair_t[:].rearrange("p (r c) t -> p r c t", c=PITCH)
-        zeros = const.tile([P, PITCH + 1, 2], F32, name="zeros")
-        nc.vector.memset(zeros[:], 0.0)
-        for grid in xt_grid:
-            nc.scalar.copy(out=grid[:, 0, :, :], in_=zeros[:, 0:PITCH, :])
-            nc.scalar.copy(out=grid[:, :, 0, :], in_=zeros[:])
+        def mark(tile, fill, base, step_y, step_x):
+            nc.gpsimd.affine_select(
+                out=tile[:],
+                in_=tile[:],
+                pattern=[[step_y, STRIP], [step_x, WINDOW]],
+                compare_op=NOT_EQUAL,
+                fill=fill,
+                base=base,
+                channel_multiplier=1,
+            )
 
-        def transpose(g):
-            bi, i0 = place(g)
-            x_words = x_tiles[g][:].bitcast(F32)
-            for h in range(BAND // BANK_ROWS):
-                row = i0 + h * BANK_ROWS
-                xT = psum_tr.tile([P, 2, BANK_ROWS * GRID], F32, name="xT", tag="tr")
-                for q in range(BANK_TILES):
-                    for u in range(2):
-                        nc.tensor.transpose(
-                            out=xT[:, u, q * P : (q + 1) * P],
-                            in_=x_words[:, h * BANK_TILES + q, u:WORDS:2],
-                            identity=ident[:],
-                        )
+        centre = PATCH_ROWS + 1
+        neighbours = {}
+        whole = const.tile([P, WINDOW_NODES], BF16, name="nb_mid_mid")
+        nc.gpsimd.memset(whole[:], 0.0)
+        for shift in (-1, 1, -PATCH_ROWS, PATCH_ROWS):
+            mark(whole, 1.0, -centre - shift, -1, -PATCH_ROWS)
+        neighbours[("mid", "mid")] = whole
+
+        def without(source, name, base, step_y, step_x):
+            tile = const.tile([P, WINDOW_NODES], BF16, name=name)
+            nc.gpsimd.tensor_copy(out=tile[:], in_=source[:])
+            mark(tile, 0.0, base, step_y, step_x)
+            return tile
+
+        neighbours[("mid", "left")] = without(whole, "nb_mid_left", -1, -1, -FAR)
+        neighbours[("mid", "right")] = without(
+            whole, "nb_mid_right", -((PATCH_COLS - 2) * PATCH_ROWS + 1) + FAR * (WINDOW - 1), -1, -FAR
+        )
+        for side in ("left", "mid", "right"):
+            neighbours[("bottom", side)] = without(
+                neighbours[("mid", side)],
+                "nb_bottom_" + side,
+                -(2 * PATCH_ROWS - 1) + FAR * (STRIP - 1),
+                -FAR,
+                -PATCH_ROWS,
+            )
+            neighbours[("top", side)] = without(
+                neighbours[("mid", side)], "nb_top_" + side, -PATCH_ROWS, -FAR, -PATCH_ROWS
+            )
+
+        xt = [const.tile([P, XT_ROWS * PITCH, PACK], BF16, name="xt%d" % bi) for bi in range(BATCH)]
+        xt_grid = [t[:].bitcast(F32).rearrange("p (r c) u -> p r c u", c=PITCH) for t in xt]
+        pair_t = const.tile([P, PAIR_ROWS * PITCH, PACK], F32, name="pair_t")
+        pair_grid = pair_t[:].rearrange("p (r c) t -> p r c t", c=PITCH)
+        zeros = const.tile([P, PITCH, 2], F32, name="zeros")
+        nc.vector.memset(zeros[:], 0.0)
+        for bi in range(BATCH):
+            outside = 0 if bi == 0 else ADD_ROWS + 1
+            nc.scalar.copy(out=xt_grid[bi][:, outside, :, :], in_=zeros[:])
+            nc.scalar.copy(out=xt_grid[bi][:, :, 0, :], in_=zeros[:, 0:XT_ROWS, :])
+
+        def transpose_unit(kind, g):
+            x_words = x_tiles[(kind, g)][:].bitcast(F32)
+            if kind == "band":
+                bi, i0, row = place(g)
+                for h in range(BAND // BANK_ROWS):
+                    r0 = i0 + h * BANK_ROWS
+                    xT = to_scalar.tile([P, 2, BANK_ROWS * GRID], F32, name="xT", tag="s")
+                    for q in range(BANK_TILES):
+                        for u in range(2):
+                            nc.tensor.transpose(
+                                out=xT[:, u, q * P : (q + 1) * P],
+                                in_=x_words[:, h * BANK_TILES + q, u:WORDS:2],
+                                identity=ident[:],
+                            )
+                    nc.scalar.copy(
+                        out=xt_grid[bi][:, r0 + 1 : r0 + 1 + BANK_ROWS, 1:PITCH, :],
+                        in_=xT[:].rearrange("p u (r c) -> p r c u", r=BANK_ROWS),
+                    )
+            else:
+                xT = to_scalar.tile([P, 2, BANK_ROWS * GRID], F32, name="xT", tag="s")
+                for u in range(2):
+                    nc.tensor.transpose(out=xT[:, u, 0:P], in_=x_words[:, 0, u:WORDS:2], identity=ident[:])
+                at = ADD_ROWS + 1 if g == 0 else 0
+                col = 0 if g == 0 else GRID
                 nc.scalar.copy(
-                    out=xt_grid[bi][:, row + 1 : row + 1 + BANK_ROWS, 1:PITCH, :],
-                    in_=xT[:].rearrange("p u (r c) -> p r c u", r=BANK_ROWS),
+                    out=xt_grid[g][:, at : at + 1, 1:PITCH, :],
+                    in_=xT[:, :, col : col + GRID].rearrange("p u (r c) -> p r c u", r=1),
                 )
 
         def first_add(g):
-            bi, i0 = place(g)
-            first, last = i0 * PITCH, (i0 + BAND) * PITCH
+            bi, i0, row = place(g)
+            rows = BAND + 1 if i0 + BAND == ADD_ROWS else BAND
+            first, last = i0 * PITCH, (i0 + rows) * PITCH
             nc.vector.tensor_tensor(
                 out=pair_t[:, first:last, :],
                 in0=xt[bi][:, first:last, :],
                 in1=xt[bi][:, first + DIAGONAL : last + DIAGONAL, :],
                 op=ADD,
             )
-            if i0 + BAND == GRID:
-                nc.vector.tensor_copy(out=pair_t[:, last:, :], in_=xt[bi][:, last : last + PITCH, :])
 
         def second_add(g):
             i0 = place(g)[1]
@@ -160,7 +265,7 @@ def tile_graphconvlayer_kernel(tc, X, W_gcn_words, W_gcn_scales, b, H, Wd, out):
             outT = work.tile([P, F_BLOCKS, BAND_NODES], F32, name="outT")
             for f in range(F_BLOCKS):
                 cols = slice(f * P, (f + 1) * P)
-                acc = psum_mx.tile([P, BAND_NODES], F32, name="acc")
+                acc = to_scalar.tile([P, BAND_NODES], F32, name="acc", tag="s")
                 nc.tensor.matmul_mx(
                     out=acc[:],
                     lhsT=w_codes[:, cols].bitcast(FP8X4),
@@ -176,65 +281,124 @@ def tile_graphconvlayer_kernel(tc, X, W_gcn_words, W_gcn_scales, b, H, Wd, out):
             outT_tiles[g] = outT
 
         def transpose_back(g):
-            bi, i0 = place(g)
+            row = place(g)[2]
             outT = outT_tiles[g]
             for q in range(TILES):
-                back = psum_tr.tile([P, F_OUT], F32, name="back", tag="tr")
+                back = to_scalar.tile([P, F_OUT], F32, name="back", tag="s")
                 for f in range(F_BLOCKS):
                     nc.tensor.transpose(
                         out=back[:, f * P : (f + 1) * P],
                         in_=outT[:, f, q * P : (q + 1) * P],
                         identity=ident[:],
                     )
-                o_sb = stores.tile([P, F_OUT], F32, name="o_sb")
+                o_sb = stores_s.tile([P, F_OUT], F32, name="o_sb")
                 nc.scalar.copy(out=o_sb[:], in_=back[:])
-                node = i0 * GRID + q * P
-                nc.sync.dma_start(out=out[bi, node : node + P, :], in_=o_sb[:])
+                node = row * GRID + q * P
+                nc.sync.dma_start(out=out_flat[node : node + P, :], in_=o_sb[:])
 
-        def multiply_direct(g):
-            bi, i0 = place(g)
-            codes, scales = mx_tiles[g]
-            for q in range(TILES):
-                nodes = slice(q * P, (q + 1) * P)
-                acc = psum_mx.tile([P, F_OUT], F32, name="acc")
-                nc.tensor.matmul_mx(
-                    out=acc[:],
-                    lhsT=codes[:, nodes].bitcast(FP8X4),
-                    lhsT_scale=scales[:, nodes],
-                    rhs=w_codes[:].bitcast(FP8X4),
-                    rhs_scale=w_scales[:],
-                    start=True,
-                    stop=True,
+        def multiply_direct(codes, scales, q):
+            nodes = slice(q * P, (q + 1) * P)
+            acc = to_vector.tile([P, F_OUT], F32, name="acc_v", tag="v")
+            nc.tensor.matmul_mx(
+                out=acc[:],
+                lhsT=codes[:, nodes].bitcast(FP8X4),
+                lhsT_scale=scales[:, nodes],
+                rhs=w_codes[:].bitcast(FP8X4),
+                rhs_scale=w_scales[:],
+                start=True,
+                stop=True,
+            )
+            return acc
+
+        def add_bias(acc, node):
+            o_sb = stores_v.tile([P, F_OUT], F32, name="o_sb")
+            nc.vector.tensor_tensor(out=o_sb[:], in0=acc[:], in1=bias_row[:], op=ADD)
+            nc.sync.dma_start(out=out_flat[node : node + P, :], in_=o_sb[:])
+
+        def sum_strip(e):
+            row = STRIP_TOP + e * STRIP
+            level = "bottom" if row + STRIP == GRID else "top" if row == GRID else "mid"
+            ax = waiting.tile([P, STRIP, GRID, PACK], BF16, name="strip_ax", align_bytes=64)
+            for h in range(PATCHES):
+                side = "left" if h == 0 else "right" if h == PATCHES - 1 else "mid"
+                xk = patch_tiles[(e, h)]
+                sums = to_scalar.tile([P, PACK, P], F32, name="sums", tag="s")
+                for t in range(PACK):
+                    nc.tensor.matmul(
+                        out=sums[:, t, 0:WINDOW_NODES],
+                        lhsT=xk[:, t:F_IN:PACK],
+                        rhs=neighbours[(level, side)][:],
+                        start=True,
+                        stop=True,
+                    )
+                col = window_col(h)
+                nc.scalar.copy(
+                    out=ax[:, :, col : col + WINDOW, :],
+                    in_=sums[:, :, 0:WINDOW_NODES].rearrange("p t (y x) -> p y x t", x=WINDOW),
                 )
-                o_sb = stores.tile([P, F_OUT], F32, name="o_sb")
-                nc.vector.tensor_tensor(out=o_sb[:], in0=acc[:], in1=bias_row[:], op=ADD)
-                node = i0 * GRID + q * P
-                nc.sync.dma_start(out=out[bi, node : node + P, :], in_=o_sb[:])
+            strip_ax[e] = ax
 
-        ctx.enter_context(tc.manual_schedule())
+        def quantise_strip(e):
+            codes = work.tile([P, STRIP_NODES], U32, name="strip_codes", align_bytes=64)
+            scales = work.tile([P, STRIP_NODES], U8, name="strip_scales", align_bytes=64)
+            flat = strip_ax[e][:].rearrange("p r c t -> p (r c t)")
+            for lo, hi in ((0, 2 * P), (2 * P, 3 * P)):
+                nc.vector.quantize_mx(
+                    out=codes[:, lo:hi].bitcast(FP8X4),
+                    scales=scales[:, lo:hi],
+                    in_=flat[:, lo * PACK : hi * PACK],
+                )
+            strip_mx[e] = (codes, scales)
 
-        def fill_xt(g):
-            if g < BANDS:
-                transpose(g)
-            if g + LOADS_AHEAD < BANDS:
-                load(g + LOADS_AHEAD)
+        if MANUAL:
+            ctx.enter_context(tc.manual_schedule())
 
-        fill_xt(0)
+        transpose_unit("band", 0)
         transpose_bias()
-        for g in range(1, XT_AHEAD):
-            fill_xt(g)
+        for g in range(1, 4):
+            transpose_unit("band", g)
+        sum_strip(0)
+        sum_strip(1)
+        transpose_unit("band", 4)
+        sum_strip(2)
+        load_unit("edge", 0)
+        load_unit("edge", 1)
+        load_unit("band", BANDS_AHEAD)
+        load_strip(STRIPS_AHEAD)
+
         turned = BANDS - DIRECT_BANDS
         for step in range(BANDS + 2):
+            g = step - 2
             if step < BANDS:
                 first_add(step)
-            if 0 <= step - 2 < BANDS:
-                quantise(step - 2)
-            if 0 <= step - 2 < turned:
-                multiply(step - 2)
-            if turned <= step - 2 < BANDS:
-                multiply_direct(step - 2)
-            if 0 <= step - 3 < turned:
-                transpose_back(step - 3)
-            fill_xt(step + XT_AHEAD)
+            if 0 <= g - 1 < turned:
+                transpose_back(g - 1)
+            products = []
+            if 0 <= g < STRIPS:
+                quantise_strip(g)
+            if 0 <= g < BANDS:
+                quantise(g)
+            if 0 <= g < STRIPS:
+                codes, scales = strip_mx[g]
+                products = [multiply_direct(codes, scales, q) for q in range(STRIP_TILES)]
+            if 0 <= g < turned:
+                multiply(g)
             if 0 <= step - 1 < BANDS:
                 second_add(step - 1)
+            for q in range(len(products)):
+                add_bias(products[q], (STRIP_TOP + g * STRIP) * GRID + q * P)
+            if turned <= g < BANDS:
+                codes, scales = mx_tiles[g]
+                for q in range(TILES):
+                    add_bias(multiply_direct(codes, scales, q), place(g)[2] * GRID + q * P)
+            if g == 0:
+                transpose_unit("edge", 0)
+                transpose_unit("edge", 1)
+            if 0 <= g and g + BANDS_AHEAD < BANDS:
+                transpose_unit("band", g + BANDS_AHEAD)
+            if 0 <= g and g + STRIPS_AHEAD < STRIPS:
+                sum_strip(g + STRIPS_AHEAD)
+            if 0 <= g and g + BANDS_AHEAD + 1 < BANDS:
+                load_unit("band", g + BANDS_AHEAD + 1)
+            if 0 <= g and g + STRIPS_AHEAD + 1 < STRIPS:
+                load_strip(g + STRIPS_AHEAD + 1)

@@ -45,8 +45,8 @@ WINDOW_NODES = STRIP * WINDOW
 PATCHES = 5
 FAR = 1000
 
-BANDS_AHEAD = 5
-STRIPS_AHEAD = 3
+BANDS_AHEAD = 4
+STRIPS_AHEAD = 2
 DIRECT_BANDS = 1
 
 FLOPS = 2 * BATCH * GRID * GRID * F_IN * F_OUT
@@ -60,8 +60,8 @@ def tile_graphconvlayer_kernel(tc, X, W_gcn_words, W_gcn_scales, b, H, Wd, out):
 
     with ExitStack() as ctx:
         const = ctx.enter_context(tc.tile_pool(name="const", bufs=1))
-        loads = ctx.enter_context(tc.tile_pool(name="loads", bufs=BANDS_AHEAD))
-        patches = ctx.enter_context(tc.tile_pool(name="patches", bufs=STRIPS_AHEAD * PATCHES))
+        loads = ctx.enter_context(tc.tile_pool(name="loads", bufs=BANDS_AHEAD + 1))
+        patches = ctx.enter_context(tc.tile_pool(name="patches", bufs=(STRIPS_AHEAD + 1) * PATCHES))
         work = ctx.enter_context(tc.tile_pool(name="work", bufs=3))
         waiting = ctx.enter_context(tc.tile_pool(name="waiting", bufs=STRIPS_AHEAD + 2))
         stores_s = ctx.enter_context(tc.tile_pool(name="stores_s", bufs=6))
@@ -109,9 +109,10 @@ def tile_graphconvlayer_kernel(tc, X, W_gcn_words, W_gcn_scales, b, H, Wd, out):
                 )
                 patch_tiles[(e, h)] = xk
 
-        for g in range(4):
+        for g in range(3):
             load_unit("band", g)
         load_strip(0)
+        load_unit("band", 3)
         ident = const.tile([P, P], F32, name="ident")
         make_identity(nc, ident[:])
 
@@ -130,6 +131,8 @@ def tile_graphconvlayer_kernel(tc, X, W_gcn_words, W_gcn_scales, b, H, Wd, out):
         load_strip(1)
         load_unit("band", 4)
         load_strip(2)
+        load_unit("edge", 0)
+        load_unit("edge", 1)
 
         b_rows = const.tile([P, P], BF16, name="b_rows")
         nc.vector.memset(b_rows[:].bitcast(F32), 0.0)
@@ -355,20 +358,19 @@ def tile_graphconvlayer_kernel(tc, X, W_gcn_words, W_gcn_scales, b, H, Wd, out):
 
         transpose_unit("band", 0)
         transpose_bias()
-        for g in range(1, 4):
-            transpose_unit("band", g)
+        transpose_unit("band", 1)
+        transpose_unit("band", 2)
         sum_strip(0)
+        transpose_unit("band", 3)
         sum_strip(1)
-        transpose_unit("band", 4)
-        sum_strip(2)
-        load_unit("edge", 0)
-        load_unit("edge", 1)
-        load_unit("band", BANDS_AHEAD)
-        load_strip(STRIPS_AHEAD)
 
         turned = BANDS - DIRECT_BANDS
         for step in range(BANDS + 2):
             g = step - 2
+            if 0 <= g and g + BANDS_AHEAD + 1 < BANDS:
+                load_unit("band", g + BANDS_AHEAD + 1)
+            if 0 <= g and g + STRIPS_AHEAD + 1 < STRIPS:
+                load_strip(g + STRIPS_AHEAD + 1)
             if step < BANDS:
                 first_add(step)
             if 0 <= g - 1 < turned:
@@ -398,7 +400,3 @@ def tile_graphconvlayer_kernel(tc, X, W_gcn_words, W_gcn_scales, b, H, Wd, out):
                 transpose_unit("band", g + BANDS_AHEAD)
             if 0 <= g and g + STRIPS_AHEAD < STRIPS:
                 sum_strip(g + STRIPS_AHEAD)
-            if 0 <= g and g + BANDS_AHEAD + 1 < BANDS:
-                load_unit("band", g + BANDS_AHEAD + 1)
-            if 0 <= g and g + STRIPS_AHEAD + 1 < STRIPS:
-                load_strip(g + STRIPS_AHEAD + 1)

@@ -140,15 +140,22 @@ def tile_graphconvlayer_kernel(tc, X, W_gcn_words, W_gcn_scales, b, H, Wd, out):
         b_rows_f32 = const.tile([P, P], F32, name="b_rows_f32")
         nc.vector.tensor_copy(out=b_rows_f32[:], in_=b_rows[:])
         bias_col = const.tile([P, F_BLOCKS], F32, name="bias_col")
-        bias_row_bf = const.tile([P, F_OUT], BF16, name="bias_row_bf")
-        nc.scalar.dma_start(out=bias_row_bf[:], in_=b.partition_broadcast(P))
+        b_first = const.tile([P, F_OUT], BF16, name="b_first")
+        nc.vector.memset(b_first[:].bitcast(F32), 0.0)
+        nc.scalar.dma_start(out=b_first[0:1, :], in_=b.rearrange("(o f) -> o f", o=1))
+        ones = const.tile([P, P], BF16, name="ones")
+        nc.vector.memset(ones[:], 1.0)
         bias_row = const.tile([P, F_OUT], F32, name="bias_row")
-        nc.vector.tensor_copy(out=bias_row[:], in_=bias_row_bf[:])
 
         def transpose_bias():
             b_ps = to_vector.tile([P, F_OUT], F32, name="b_ps", tag="v")
             nc.tensor.transpose(out=b_ps[:, 0:P], in_=b_rows_f32[:], identity=ident[:])
             nc.vector.tensor_copy(out=bias_col[:], in_=b_ps[:, 0:F_BLOCKS])
+
+        def spread_bias():
+            row_ps = to_vector.tile([P, F_OUT], F32, name="row_ps", tag="v")
+            nc.tensor.matmul(out=row_ps[:], lhsT=ones[:], rhs=b_first[:], start=True, stop=True)
+            nc.scalar.copy(out=bias_row[:], in_=row_ps[:])
 
         def mark(tile, fill, base, step_y, step_x):
             nc.gpsimd.affine_select(
@@ -364,6 +371,7 @@ def tile_graphconvlayer_kernel(tc, X, W_gcn_words, W_gcn_scales, b, H, Wd, out):
         transpose_unit("band", 3)
         sum_strip(1)
 
+        spread_bias()
         turned = BANDS - DIRECT_BANDS
         for step in range(BANDS + 2):
             g = step - 2

@@ -47,7 +47,7 @@ FAR = 1000
 
 BANDS_AHEAD = 4
 STRIPS_AHEAD = 2
-DIRECT_BANDS = 1
+DIRECT_BANDS = 2
 
 FLOPS = 2 * BATCH * GRID * GRID * F_IN * F_OUT
 

@@ -40,9 +40,9 @@ STRIPS = (BATCH * GRID - BATCH * ADD_ROWS) // STRIP
 STRIP_NODES = STRIP * GRID
 STRIP_TILES = STRIP_NODES // P
 PATCH_ROWS, PATCH_COLS = STRIP + 2, 16
-WINDOW = PATCH_COLS - 3
-WINDOW_NODES = STRIP * WINDOW
-PATCHES = 5
+WINDOWS = (14, 12, 12, 12, 14)
+PATCHES = len(WINDOWS)
+WINDOW_COL = tuple(sum(WINDOWS[:h]) for h in range(PATCHES))
 FAR = 1000
 
 BANDS_AHEAD = 4
@@ -93,13 +93,10 @@ def tile_graphconvlayer_kernel(tc, X, W_gcn_words, W_gcn_scales, b, H, Wd, out):
                 )
             x_tiles[(kind, g)] = x_sb
 
-        def window_col(h):
-            return min(h * WINDOW, GRID - WINDOW)
-
         def load_strip(e):
             row = STRIP_TOP + e * STRIP
             for h in range(PATCHES):
-                first = (row - 1) * GRID + window_col(h) - 1
+                first = (row - 1) * GRID + WINDOW_COL[h] - 1
                 xk = patches.tile([P, F_IN], BF16, name="xk")
                 nc.sync.dma_start(
                     out=xk[:],
@@ -157,45 +154,50 @@ def tile_graphconvlayer_kernel(tc, X, W_gcn_words, W_gcn_scales, b, H, Wd, out):
             nc.tensor.matmul(out=row_ps[:], lhsT=ones[:], rhs=b_first[:], start=True, stop=True)
             nc.scalar.copy(out=bias_row[:], in_=row_ps[:])
 
-        def mark(tile, fill, base, step_y, step_x):
+        def mark(tile, width, fill, base, step_y, step_x):
             nc.gpsimd.affine_select(
                 out=tile[:],
                 in_=tile[:],
-                pattern=[[step_y, STRIP], [step_x, WINDOW]],
+                pattern=[[step_y, STRIP], [step_x, width]],
                 compare_op=NOT_EQUAL,
                 fill=fill,
                 base=base,
                 channel_multiplier=1,
             )
 
-        centre = PATCH_ROWS + 1
-        neighbours = {}
-        whole = const.tile([P, WINDOW_NODES], BF16, name="nb_mid_mid")
-        nc.gpsimd.memset(whole[:], 0.0)
-        for shift in (-1, 1, -PATCH_ROWS, PATCH_ROWS):
-            mark(whole, 1.0, -centre - shift, -1, -PATCH_ROWS)
-        neighbours[("mid", "mid")] = whole
-
-        def without(source, name, base, step_y, step_x):
-            tile = const.tile([P, WINDOW_NODES], BF16, name=name)
-            nc.gpsimd.tensor_copy(out=tile[:], in_=source[:])
-            mark(tile, 0.0, base, step_y, step_x)
+        def all_four(name, width):
+            tile = const.tile([P, STRIP * width], BF16, name=name)
+            nc.gpsimd.memset(tile[:], 0.0)
+            for shift in (-1, 1, -PATCH_ROWS, PATCH_ROWS):
+                mark(tile, width, 1.0, -(PATCH_ROWS + 1) - shift, -1, -PATCH_ROWS)
             return tile
 
-        neighbours[("mid", "left")] = without(whole, "nb_mid_left", -1, -1, -FAR)
-        neighbours[("mid", "right")] = without(
-            whole, "nb_mid_right", -((PATCH_COLS - 2) * PATCH_ROWS + 1) + FAR * (WINDOW - 1), -1, -FAR
-        )
-        for side in ("left", "mid", "right"):
+        def without(source, name, width, base, step_y, step_x):
+            tile = const.tile([P, STRIP * width], BF16, name=name)
+            nc.gpsimd.tensor_copy(out=tile[:], in_=source[:])
+            mark(tile, width, 0.0, base, step_y, step_x)
+            return tile
+
+        wide, narrow = WINDOWS[0], WINDOWS[1]
+        inner = all_four("nb_inner", wide)
+        neighbours = {
+            ("mid", "left"): without(inner, "nb_mid_left", wide, -1, -1, -FAR),
+            ("mid", "mid"): all_four("nb_mid_mid", narrow),
+            ("mid", "right"): without(
+                inner, "nb_mid_right", wide, -((wide + 1) * PATCH_ROWS + 1) + FAR * (wide - 1), -1, -FAR
+            ),
+        }
+        for side, width in (("left", wide), ("mid", narrow), ("right", wide)):
             neighbours[("bottom", side)] = without(
                 neighbours[("mid", side)],
                 "nb_bottom_" + side,
+                width,
                 -(2 * PATCH_ROWS - 1) + FAR * (STRIP - 1),
                 -FAR,
                 -PATCH_ROWS,
             )
             neighbours[("top", side)] = without(
-                neighbours[("mid", side)], "nb_top_" + side, -PATCH_ROWS, -FAR, -PATCH_ROWS
+                neighbours[("mid", side)], "nb_top_" + side, width, -PATCH_ROWS, -FAR, -PATCH_ROWS
             )
 
         xt = [const.tile([P, XT_ROWS * PITCH, PACK], BF16, name="xt%d" % bi) for bi in range(BATCH)]
@@ -333,18 +335,19 @@ def tile_graphconvlayer_kernel(tc, X, W_gcn_words, W_gcn_scales, b, H, Wd, out):
                 side = "left" if h == 0 else "right" if h == PATCHES - 1 else "mid"
                 xk = patch_tiles[(e, h)]
                 sums = to_scalar.tile([P, PACK, P], F32, name="sums", tag="s")
+                nodes = STRIP * WINDOWS[h]
                 for t in range(PACK):
                     nc.tensor.matmul(
-                        out=sums[:, t, 0:WINDOW_NODES],
+                        out=sums[:, t, 0:nodes],
                         lhsT=xk[:, t:F_IN:PACK],
                         rhs=neighbours[(level, side)][:],
                         start=True,
                         stop=True,
                     )
-                col = window_col(h)
+                col = WINDOW_COL[h]
                 nc.scalar.copy(
-                    out=ax[:, :, col : col + WINDOW, :],
-                    in_=sums[:, :, 0:WINDOW_NODES].rearrange("p t (y x) -> p y x t", x=WINDOW),
+                    out=ax[:, :, col : col + WINDOWS[h], :],
+                    in_=sums[:, :, 0:nodes].rearrange("p t (y x) -> p y x t", x=WINDOWS[h]),
                 )
             strip_ax[e] = ax
 

@@ -13,8 +13,6 @@ ADD = mybir.AluOpType.add
 NOT_EQUAL = mybir.AluOpType.not_equal
 IDENTITY = mybir.ActivationFunctionType.Identity
 
-MANUAL = True
-
 P = 128
 PACK = 4
 BATCH, GRID, F_IN, F_OUT = 2, 64, 512, 512
@@ -42,6 +40,7 @@ STRIP_TILES = STRIP_NODES // P
 PATCH_ROWS, PATCH_COLS = STRIP + 2, 16
 WINDOWS = (14, 12, 12, 12, 14)
 PATCHES = len(WINDOWS)
+WIDEST = max(WINDOWS)
 WINDOW_COL = tuple(sum(WINDOWS[:h]) for h in range(PATCHES))
 FAR = 1000
 
@@ -64,8 +63,8 @@ def tile_graphconvlayer_kernel(tc, X, W_gcn_words, W_gcn_scales, b, H, Wd, out):
         patches = ctx.enter_context(tc.tile_pool(name="patches", bufs=(STRIPS_AHEAD + 1) * PATCHES))
         work = ctx.enter_context(tc.tile_pool(name="work", bufs=3))
         waiting = ctx.enter_context(tc.tile_pool(name="waiting", bufs=STRIPS_AHEAD + 2))
-        stores_s = ctx.enter_context(tc.tile_pool(name="stores_s", bufs=6))
-        stores_v = ctx.enter_context(tc.tile_pool(name="stores_v", bufs=5))
+        stores_s = ctx.enter_context(tc.tile_pool(name="stores_s", bufs=5))
+        stores_v = ctx.enter_context(tc.tile_pool(name="stores_v", bufs=8))
         to_scalar = ctx.enter_context(tc.psum_pool(name="to_scalar", bufs=5))
         to_vector = ctx.enter_context(tc.psum_pool(name="to_vector", bufs=3))
 
@@ -80,10 +79,13 @@ def tile_graphconvlayer_kernel(tc, X, W_gcn_words, W_gcn_scales, b, H, Wd, out):
             if kind == "band":
                 row = place(g)[2]
                 x_sb = loads.tile([P, TILES, F_IN], BF16, name="x_sb")
-                nc.sync.dma_start(
-                    out=x_sb[:],
-                    in_=x_flat[row * GRID : (row + BAND) * GRID, :].rearrange("(q p) f -> p q f", p=P),
-                )
+                part = BANK_TILES if g == 0 else TILES
+                for q in range(0, TILES, part):
+                    node = row * GRID + q * P
+                    nc.sync.dma_start(
+                        out=x_sb[:, q : q + part, :],
+                        in_=x_flat[node : node + part * P, :].rearrange("(q p) f -> p q f", p=P),
+                    )
             else:
                 row = ADD_ROWS if g == 0 else ADD_TOP[1] - 2
                 x_sb = loads.tile([P, 1, F_IN], BF16, name="x_edge")
@@ -135,7 +137,6 @@ def tile_graphconvlayer_kernel(tc, X, W_gcn_words, W_gcn_scales, b, H, Wd, out):
         nc.vector.memset(b_rows[:].bitcast(F32), 0.0)
         nc.scalar.dma_start(out=b_rows[0:F_BLOCKS, :], in_=b.rearrange("(f p) -> f p", p=P))
         b_rows_f32 = const.tile([P, P], F32, name="b_rows_f32")
-        nc.vector.tensor_copy(out=b_rows_f32[:], in_=b_rows[:])
         bias_col = const.tile([P, F_BLOCKS], F32, name="bias_col")
         b_first = const.tile([P, F_OUT], BF16, name="b_first")
         nc.vector.memset(b_first[:].bitcast(F32), 0.0)
@@ -145,59 +146,54 @@ def tile_graphconvlayer_kernel(tc, X, W_gcn_words, W_gcn_scales, b, H, Wd, out):
         bias_row = const.tile([P, F_OUT], F32, name="bias_row")
 
         def transpose_bias():
+            nc.scalar.copy(out=b_rows_f32[:], in_=b_rows[:])
             b_ps = to_vector.tile([P, F_OUT], F32, name="b_ps", tag="v")
             nc.tensor.transpose(out=b_ps[:, 0:P], in_=b_rows_f32[:], identity=ident[:])
-            nc.vector.tensor_copy(out=bias_col[:], in_=b_ps[:, 0:F_BLOCKS])
+            nc.scalar.copy(out=bias_col[:], in_=b_ps[:, 0:F_BLOCKS])
 
         def spread_bias():
             row_ps = to_vector.tile([P, F_OUT], F32, name="row_ps", tag="v")
             nc.tensor.matmul(out=row_ps[:], lhsT=ones[:], rhs=b_first[:], start=True, stop=True)
             nc.scalar.copy(out=bias_row[:], in_=row_ps[:])
 
-        def mark(tile, width, fill, base, step_y, step_x):
+        def mark(tile, fill, base, step_y, step_x):
             nc.gpsimd.affine_select(
                 out=tile[:],
                 in_=tile[:],
-                pattern=[[step_y, STRIP], [step_x, width]],
+                pattern=[[step_y, STRIP], [step_x, WIDEST]],
                 compare_op=NOT_EQUAL,
                 fill=fill,
                 base=base,
                 channel_multiplier=1,
             )
 
-        def all_four(name, width):
-            tile = const.tile([P, STRIP * width], BF16, name=name)
-            nc.gpsimd.memset(tile[:], 0.0)
-            for shift in (-1, 1, -PATCH_ROWS, PATCH_ROWS):
-                mark(tile, width, 1.0, -(PATCH_ROWS + 1) - shift, -1, -PATCH_ROWS)
-            return tile
-
-        def without(source, name, width, base, step_y, step_x):
-            tile = const.tile([P, STRIP * width], BF16, name=name)
+        def without(source, name, base, step_y, step_x):
+            tile = const.tile([P, STRIP * WIDEST], BF16, name=name)
             nc.gpsimd.tensor_copy(out=tile[:], in_=source[:])
-            mark(tile, width, 0.0, base, step_y, step_x)
+            mark(tile, 0.0, base, step_y, step_x)
             return tile
 
-        wide, narrow = WINDOWS[0], WINDOWS[1]
-        inner = all_four("nb_inner", wide)
+        inner = const.tile([P, STRIP * WIDEST], BF16, name="nb_inner")
+        nc.gpsimd.memset(inner[:], 0.0)
+        for shift in (-1, 1, -PATCH_ROWS, PATCH_ROWS):
+            mark(inner, 1.0, -(PATCH_ROWS + 1) - shift, -1, -PATCH_ROWS)
         neighbours = {
-            ("mid", "left"): without(inner, "nb_mid_left", wide, -1, -1, -FAR),
-            ("mid", "mid"): all_four("nb_mid_mid", narrow),
+            ("mid", "left"): without(inner, "nb_mid_left", -1, -1, -FAR),
+            ("mid", "mid"): inner,
             ("mid", "right"): without(
-                inner, "nb_mid_right", wide, -((wide + 1) * PATCH_ROWS + 1) + FAR * (wide - 1), -1, -FAR
+                inner, "nb_mid_right", -((WIDEST + 1) * PATCH_ROWS + 1) + FAR * (WIDEST - 1), -1, -FAR
             ),
         }
-        for side, width in (("left", wide), ("mid", narrow), ("right", wide)):
+        for side in ("left", "mid", "right"):
             neighbours[("bottom", side)] = without(
                 neighbours[("mid", side)],
                 "nb_bottom_" + side,
-                width,
                 -(2 * PATCH_ROWS - 1) + FAR * (STRIP - 1),
                 -FAR,
                 -PATCH_ROWS,
             )
             neighbours[("top", side)] = without(
-                neighbours[("mid", side)], "nb_top_" + side, width, -PATCH_ROWS, -FAR, -PATCH_ROWS
+                neighbours[("mid", side)], "nb_top_" + side, -PATCH_ROWS, -FAR, -PATCH_ROWS
             )
 
         xt = [const.tile([P, XT_ROWS * PITCH, PACK], BF16, name="xt%d" % bi) for bi in range(BATCH)]
@@ -243,13 +239,15 @@ def tile_graphconvlayer_kernel(tc, X, W_gcn_words, W_gcn_scales, b, H, Wd, out):
         def first_add(g):
             bi, i0, row = place(g)
             rows = BAND + 1 if i0 + BAND == ADD_ROWS else BAND
-            first, last = i0 * PITCH, (i0 + rows) * PITCH
-            nc.vector.tensor_tensor(
-                out=pair_t[:, first:last, :],
-                in0=xt[bi][:, first:last, :],
-                in1=xt[bi][:, first + DIAGONAL : last + DIAGONAL, :],
-                op=ADD,
-            )
+            cuts = (0, BANK_ROWS - 1, rows) if g == 0 else (0, rows)
+            for top, bottom in zip(cuts[:-1], cuts[1:]):
+                first, last = (i0 + top) * PITCH, (i0 + bottom) * PITCH
+                nc.vector.tensor_tensor(
+                    out=pair_t[:, first:last, :],
+                    in0=xt[bi][:, first:last, :],
+                    in1=xt[bi][:, first + DIAGONAL : last + DIAGONAL, :],
+                    op=ADD,
+                )
 
         def second_add(g):
             i0 = place(g)[1]
@@ -338,9 +336,11 @@ def tile_graphconvlayer_kernel(tc, X, W_gcn_words, W_gcn_scales, b, H, Wd, out):
                 nodes = STRIP * WINDOWS[h]
                 for t in range(PACK):
                     nc.tensor.matmul(
-                        out=sums[:, t, 0:nodes],
+                        out=sums[:, t, 0:nodes].rearrange("p (y x) -> p y x", x=WINDOWS[h]),
                         lhsT=xk[:, t:F_IN:PACK],
-                        rhs=neighbours[(level, side)][:],
+                        rhs=neighbours[(level, side)][:].rearrange("p (y x) -> p y x", x=WIDEST)[
+                            :, :, 0 : WINDOWS[h]
+                        ],
                         start=True,
                         stop=True,
                     )
@@ -363,51 +363,51 @@ def tile_graphconvlayer_kernel(tc, X, W_gcn_words, W_gcn_scales, b, H, Wd, out):
                 )
             strip_mx[e] = (codes, scales)
 
-        if MANUAL:
-            ctx.enter_context(tc.manual_schedule())
+        ctx.enter_context(tc.manual_schedule())
 
         transpose_unit("band", 0)
-        transpose_bias()
         transpose_unit("band", 1)
         transpose_unit("band", 2)
         sum_strip(0)
+        first_add(0)
+        first_add(1)
+        second_add(0)
         transpose_unit("band", 3)
-        sum_strip(1)
-
+        transpose_bias()
         spread_bias()
         turned = BANDS - DIRECT_BANDS
-        for step in range(BANDS + 2):
-            g = step - 2
-            if 0 <= g and g + BANDS_AHEAD + 1 < BANDS:
+        for g in range(BANDS):
+            strip_node = (STRIP_TOP + g * STRIP) * GRID
+            if g + BANDS_AHEAD + 1 < BANDS:
                 load_unit("band", g + BANDS_AHEAD + 1)
-            if 0 <= g and g + STRIPS_AHEAD + 1 < STRIPS:
+            if g + STRIPS_AHEAD + 1 < STRIPS:
                 load_strip(g + STRIPS_AHEAD + 1)
-            if step < BANDS:
-                first_add(step)
-            if 0 <= g - 1 < turned:
-                transpose_back(g - 1)
-            products = []
-            if 0 <= g < STRIPS:
+            if g < STRIPS:
                 quantise_strip(g)
-            if 0 <= g < BANDS:
-                quantise(g)
-            if 0 <= g < STRIPS:
-                codes, scales = strip_mx[g]
-                products = [multiply_direct(codes, scales, q) for q in range(STRIP_TILES)]
-            if 0 <= g < turned:
+                products = [multiply_direct(*strip_mx[g], q) for q in range(STRIP_TILES - 1)]
+            quantise(g)
+            if g + 2 < BANDS:
+                first_add(g + 2)
+            if g < turned:
                 multiply(g)
-            if 0 <= step - 1 < BANDS:
-                second_add(step - 1)
-            for q in range(len(products)):
-                add_bias(products[q], (STRIP_TOP + g * STRIP) * GRID + q * P)
-            if turned <= g < BANDS:
-                codes, scales = mx_tiles[g]
-                for q in range(TILES):
-                    add_bias(multiply_direct(codes, scales, q), place(g)[2] * GRID + q * P)
+            if g < STRIPS:
+                add_bias(products[0], strip_node)
+                products.append(multiply_direct(*strip_mx[g], STRIP_TILES - 1))
+                add_bias(products[1], strip_node + P)
             if g == 0:
+                sum_strip(1)
                 transpose_unit("edge", 0)
                 transpose_unit("edge", 1)
-            if 0 <= g and g + BANDS_AHEAD < BANDS:
-                transpose_unit("band", g + BANDS_AHEAD)
-            if 0 <= g and g + STRIPS_AHEAD < STRIPS:
+            if g + STRIPS_AHEAD < STRIPS:
                 sum_strip(g + STRIPS_AHEAD)
+            if 0 <= g - 1 < turned:
+                transpose_back(g - 1)
+            if g + 1 < BANDS:
+                second_add(g + 1)
+            if g + BANDS_AHEAD < BANDS:
+                transpose_unit("band", g + BANDS_AHEAD)
+            if g < STRIPS:
+                add_bias(products[2], strip_node + 2 * P)
+            if g >= turned:
+                for q in range(TILES):
+                    add_bias(multiply_direct(*mx_tiles[g], q), place(g)[2] * GRID + q * P)

from contextlib import ExitStack

import concourse.mybir as mybir
from concourse.masks import make_identity

BF16 = mybir.dt.bfloat16
F32 = mybir.dt.float32
I32 = mybir.dt.int32
U8 = mybir.dt.uint8
U32 = mybir.dt.uint32
FP8X4 = mybir.dt.float8_e4m3fn_x4
ADD = mybir.AluOpType.add
NOT_EQUAL = mybir.AluOpType.not_equal
IDENTITY = mybir.ActivationFunctionType.Identity

P = 128
PACK = 4
BATCH, GRID, F_IN, F_OUT = 2, 64, 512, 512
PITCH = GRID + 1
DIAGONAL = PITCH + 1
BAND = 8
BAND_NODES = BAND * GRID
TILES = BAND_NODES // P
F_BLOCKS = F_OUT // P
BANK_ROWS = 4
BANK_TILES = BANK_ROWS * GRID // P
WORDS = F_IN // 2

ADD_ROWS = 40
ADD_BANDS = ADD_ROWS // BAND
BANDS = BATCH * ADD_BANDS
ADD_TOP = (0, GRID + GRID - ADD_ROWS)
XT_ROWS = ADD_ROWS + 3
PAIR_ROWS = ADD_ROWS + 1
STRIP = 6
STRIP_TOP = ADD_ROWS
STRIPS = (BATCH * GRID - BATCH * ADD_ROWS) // STRIP
STRIP_NODES = STRIP * GRID
STRIP_TILES = STRIP_NODES // P
PATCH_ROWS, PATCH_COLS = STRIP + 2, 16
WINDOWS = (14, 12, 12, 12, 14)
PATCHES = len(WINDOWS)
WIDEST = max(WINDOWS)
WINDOW_COL = tuple(sum(WINDOWS[:h]) for h in range(PATCHES))
FAR = 1000

BANDS_AHEAD = 4
STRIPS_AHEAD = 2
DIRECT_BANDS = 2

FLOPS = 2 * BATCH * GRID * GRID * F_IN * F_OUT


def tile_graphconvlayer_kernel(tc, X, W_gcn_words, W_gcn_scales, b, H, Wd, out):
    nc = tc.nc
    assert (H, Wd) == (GRID, GRID)
    x_flat = X.rearrange("b n f -> (b n) f")
    out_flat = out.rearrange("b n f -> (b n) f")

    with ExitStack() as ctx:
        const = ctx.enter_context(tc.tile_pool(name="const", bufs=1))
        loads = ctx.enter_context(tc.tile_pool(name="loads", bufs=BANDS_AHEAD + 1))
        patches = ctx.enter_context(tc.tile_pool(name="patches", bufs=(STRIPS_AHEAD + 1) * PATCHES))
        work = ctx.enter_context(tc.tile_pool(name="work", bufs=3))
        waiting = ctx.enter_context(tc.tile_pool(name="waiting", bufs=STRIPS_AHEAD + 2))
        stores_s = ctx.enter_context(tc.tile_pool(name="stores_s", bufs=5))
        stores_v = ctx.enter_context(tc.tile_pool(name="stores_v", bufs=8))
        to_scalar = ctx.enter_context(tc.psum_pool(name="to_scalar", bufs=5))
        to_vector = ctx.enter_context(tc.psum_pool(name="to_vector", bufs=3))

        x_tiles, ax_tiles, mx_tiles, outT_tiles = {}, {}, {}, {}
        patch_tiles, strip_ax, strip_mx = {}, {}, {}

        def place(g):
            bi, i0 = g // ADD_BANDS, g % ADD_BANDS * BAND
            return bi, i0, ADD_TOP[bi] + i0

        def load_unit(kind, g):
            if kind == "band":
                row = place(g)[2]
                x_sb = loads.tile([P, TILES, F_IN], BF16, name="x_sb")
                part = BANK_TILES if g == 0 else TILES
                for q in range(0, TILES, part):
                    node = row * GRID + q * P
                    nc.sync.dma_start(
                        out=x_sb[:, q : q + part, :],
                        in_=x_flat[node : node + part * P, :].rearrange("(q p) f -> p q f", p=P),
                    )
            else:
                row = ADD_ROWS if g == 0 else ADD_TOP[1] - 2
                x_sb = loads.tile([P, 1, F_IN], BF16, name="x_edge")
                nc.sync.dma_start(
                    out=x_sb[:],
                    in_=x_flat[row * GRID : (row + 2) * GRID, :].rearrange("(q p) f -> p q f", p=P),
                )
            x_tiles[(kind, g)] = x_sb

        def load_strip(e):
            row = STRIP_TOP + e * STRIP
            for h in range(PATCHES):
                first = (row - 1) * GRID + WINDOW_COL[h] - 1
                xk = patches.tile([P, F_IN], BF16, name="xk")
                nc.sync.dma_start(
                    out=xk[:],
                    in_=x_flat[first : first + PATCH_ROWS * GRID, :].rearrange("(r c) f -> c r f", c=GRID)[
                        0:PATCH_COLS, :, :
                    ],
                )
                patch_tiles[(e, h)] = xk

        for g in range(3):
            load_unit("band", g)
        load_strip(0)
        load_unit("band", 3)
        ident = const.tile([P, P], F32, name="ident")
        make_identity(nc, ident[:])

        w_codes = const.tile([P, F_OUT], U32, name="w_codes", align_bytes=64)
        nc.sync.dma_start(
            out=w_codes[:].bitcast(I32),
            in_=W_gcn_words[0].rearrange("p n t -> p (n t)").bitcast(I32),
        )
        w_scales = const.tile([P, F_OUT], U8, name="w_scales", align_bytes=64)
        nc.vector.memset(w_scales[:].bitcast(I32), 0)
        for quad in range(4):
            nc.sync.dma_start(
                out=w_scales[32 * quad : 32 * quad + 4, :].bitcast(I32),
                in_=W_gcn_scales[0, 4 * quad : 4 * quad + 4, :].bitcast(I32),
            )
        load_strip(1)
        load_unit("band", 4)
        load_strip(2)
        load_unit("edge", 0)
        load_unit("edge", 1)

        b_rows = const.tile([P, P], BF16, name="b_rows")
        nc.vector.memset(b_rows[:].bitcast(F32), 0.0)
        nc.scalar.dma_start(out=b_rows[0:F_BLOCKS, :], in_=b.rearrange("(f p) -> f p", p=P))
        b_rows_f32 = const.tile([P, P], F32, name="b_rows_f32")
        bias_col = const.tile([P, F_BLOCKS], F32, name="bias_col")
        b_first = const.tile([P, F_OUT], BF16, name="b_first")
        nc.vector.memset(b_first[:].bitcast(F32), 0.0)
        nc.scalar.dma_start(out=b_first[0:1, :], in_=b.rearrange("(o f) -> o f", o=1))
        ones = const.tile([P, P], BF16, name="ones")
        nc.vector.memset(ones[:], 1.0)
        bias_row = const.tile([P, F_OUT], F32, name="bias_row")

        def transpose_bias():
            nc.scalar.copy(out=b_rows_f32[:], in_=b_rows[:])
            b_ps = to_vector.tile([P, F_OUT], F32, name="b_ps", tag="v")
            nc.tensor.transpose(out=b_ps[:, 0:P], in_=b_rows_f32[:], identity=ident[:])
            nc.scalar.copy(out=bias_col[:], in_=b_ps[:, 0:F_BLOCKS])

        def spread_bias():
            row_ps = to_vector.tile([P, F_OUT], F32, name="row_ps", tag="v")
            nc.tensor.matmul(out=row_ps[:], lhsT=ones[:], rhs=b_first[:], start=True, stop=True)
            nc.scalar.copy(out=bias_row[:], in_=row_ps[:])

        def mark(tile, fill, base, step_y, step_x):
            nc.gpsimd.affine_select(
                out=tile[:],
                in_=tile[:],
                pattern=[[step_y, STRIP], [step_x, WIDEST]],
                compare_op=NOT_EQUAL,
                fill=fill,
                base=base,
                channel_multiplier=1,
            )

        def without(source, name, base, step_y, step_x):
            tile = const.tile([P, STRIP * WIDEST], BF16, name=name)
            nc.gpsimd.tensor_copy(out=tile[:], in_=source[:])
            mark(tile, 0.0, base, step_y, step_x)
            return tile

        inner = const.tile([P, STRIP * WIDEST], BF16, name="nb_inner")
        nc.gpsimd.memset(inner[:], 0.0)
        for shift in (-1, 1, -PATCH_ROWS, PATCH_ROWS):
            mark(inner, 1.0, -(PATCH_ROWS + 1) - shift, -1, -PATCH_ROWS)
        neighbours = {
            ("mid", "left"): without(inner, "nb_mid_left", -1, -1, -FAR),
            ("mid", "mid"): inner,
            ("mid", "right"): without(
                inner, "nb_mid_right", -((WIDEST + 1) * PATCH_ROWS + 1) + FAR * (WIDEST - 1), -1, -FAR
            ),
        }
        for side in ("left", "mid", "right"):
            neighbours[("bottom", side)] = without(
                neighbours[("mid", side)],
                "nb_bottom_" + side,
                -(2 * PATCH_ROWS - 1) + FAR * (STRIP - 1),
                -FAR,
                -PATCH_ROWS,
            )
            neighbours[("top", side)] = without(
                neighbours[("mid", side)], "nb_top_" + side, -PATCH_ROWS, -FAR, -PATCH_ROWS
            )

        xt = [const.tile([P, XT_ROWS * PITCH, PACK], BF16, name="xt%d" % bi) for bi in range(BATCH)]
        xt_grid = [t[:].bitcast(F32).rearrange("p (r c) u -> p r c u", c=PITCH) for t in xt]
        pair_t = const.tile([P, PAIR_ROWS * PITCH, PACK], F32, name="pair_t")
        pair_grid = pair_t[:].rearrange("p (r c) t -> p r c t", c=PITCH)
        zeros = const.tile([P, PITCH, 2], F32, name="zeros")
        nc.vector.memset(zeros[:], 0.0)
        for bi in range(BATCH):
            outside = 0 if bi == 0 else ADD_ROWS + 1
            nc.scalar.copy(out=xt_grid[bi][:, outside, :, :], in_=zeros[:])
            nc.scalar.copy(out=xt_grid[bi][:, :, 0, :], in_=zeros[:, 0:XT_ROWS, :])

        def transpose_unit(kind, g):
            x_words = x_tiles[(kind, g)][:].bitcast(F32)
            if kind == "band":
                bi, i0, row = place(g)
                for h in range(BAND // BANK_ROWS):
                    r0 = i0 + h * BANK_ROWS
                    xT = to_scalar.tile([P, 2, BANK_ROWS * GRID], F32, name="xT", tag="s")
                    for q in range(BANK_TILES):
                        for u in range(2):
                            nc.tensor.transpose(
                                out=xT[:, u, q * P : (q + 1) * P],
                                in_=x_words[:, h * BANK_TILES + q, u:WORDS:2],
                                identity=ident[:],
                            )
                    nc.scalar.copy(
                        out=xt_grid[bi][:, r0 + 1 : r0 + 1 + BANK_ROWS, 1:PITCH, :],
                        in_=xT[:].rearrange("p u (r c) -> p r c u", r=BANK_ROWS),
                    )
            else:
                xT = to_scalar.tile([P, 2, BANK_ROWS * GRID], F32, name="xT", tag="s")
                for u in range(2):
                    nc.tensor.transpose(out=xT[:, u, 0:P], in_=x_words[:, 0, u:WORDS:2], identity=ident[:])
                at = ADD_ROWS + 1 if g == 0 else 0
                col = 0 if g == 0 else GRID
                nc.scalar.copy(
                    out=xt_grid[g][:, at : at + 1, 1:PITCH, :],
                    in_=xT[:, :, col : col + GRID].rearrange("p u (r c) -> p r c u", r=1),
                )

        def first_add(g):
            bi, i0, row = place(g)
            rows = BAND + 1 if i0 + BAND == ADD_ROWS else BAND
            cuts = (0, BANK_ROWS - 1, rows) if g == 0 else (0, rows)
            for top, bottom in zip(cuts[:-1], cuts[1:]):
                first, last = (i0 + top) * PITCH, (i0 + bottom) * PITCH
                nc.vector.tensor_tensor(
                    out=pair_t[:, first:last, :],
                    in0=xt[bi][:, first:last, :],
                    in1=xt[bi][:, first + DIAGONAL : last + DIAGONAL, :],
                    op=ADD,
                )

        def second_add(g):
            i0 = place(g)[1]
            ax = work.tile([P, BAND, GRID, PACK], BF16, name="ax", align_bytes=64)
            nc.vector.tensor_tensor(
                out=ax[:],
                in0=pair_grid[:, i0 : i0 + BAND, 1:PITCH, :],
                in1=pair_grid[:, i0 + 1 : i0 + 1 + BAND, 0:GRID, :],
                op=ADD,
            )
            ax_tiles[g] = ax

        def quantise(g):
            codes = work.tile([P, BAND_NODES], U32, name="codes", align_bytes=64)
            scales = work.tile([P, BAND_NODES], U8, name="scales", align_bytes=64)
            nc.vector.quantize_mx(
                out=codes[:].bitcast(FP8X4),
                scales=scales[:],
                in_=ax_tiles[g][:].rearrange("p r c t -> p (r c t)"),
            )
            mx_tiles[g] = (codes, scales)

        def multiply(g):
            codes, scales = mx_tiles[g]
            outT = work.tile([P, F_BLOCKS, BAND_NODES], F32, name="outT")
            for f in range(F_BLOCKS):
                cols = slice(f * P, (f + 1) * P)
                acc = to_scalar.tile([P, BAND_NODES], F32, name="acc", tag="s")
                nc.tensor.matmul_mx(
                    out=acc[:],
                    lhsT=w_codes[:, cols].bitcast(FP8X4),
                    lhsT_scale=w_scales[:, cols],
                    rhs=codes[:].bitcast(FP8X4),
                    rhs_scale=scales[:],
                    start=True,
                    stop=True,
                )
                nc.scalar.activation(
                    out=outT[:, f, :], in_=acc[:], func=IDENTITY, bias=bias_col[:, f : f + 1], scale=1.0
                )
            outT_tiles[g] = outT

        def transpose_back(g):
            row = place(g)[2]
            outT = outT_tiles[g]
            for q in range(TILES):
                back = to_scalar.tile([P, F_OUT], F32, name="back", tag="s")
                for f in range(F_BLOCKS):
                    nc.tensor.transpose(
                        out=back[:, f * P : (f + 1) * P],
                        in_=outT[:, f, q * P : (q + 1) * P],
                        identity=ident[:],
                    )
                o_sb = stores_s.tile([P, F_OUT], F32, name="o_sb")
                nc.scalar.copy(out=o_sb[:], in_=back[:])
                node = row * GRID + q * P
                nc.sync.dma_start(out=out_flat[node : node + P, :], in_=o_sb[:])

        def multiply_direct(codes, scales, q):
            nodes = slice(q * P, (q + 1) * P)
            acc = to_vector.tile([P, F_OUT], F32, name="acc_v", tag="v")
            nc.tensor.matmul_mx(
                out=acc[:],
                lhsT=codes[:, nodes].bitcast(FP8X4),
                lhsT_scale=scales[:, nodes],
                rhs=w_codes[:].bitcast(FP8X4),
                rhs_scale=w_scales[:],
                start=True,
                stop=True,
            )
            return acc

        def add_bias(acc, node):
            o_sb = stores_v.tile([P, F_OUT], F32, name="o_sb")
            nc.vector.tensor_tensor(out=o_sb[:], in0=acc[:], in1=bias_row[:], op=ADD)
            nc.sync.dma_start(out=out_flat[node : node + P, :], in_=o_sb[:])

        def sum_strip(e):
            row = STRIP_TOP + e * STRIP
            level = "bottom" if row + STRIP == GRID else "top" if row == GRID else "mid"
            ax = waiting.tile([P, STRIP, GRID, PACK], BF16, name="strip_ax", align_bytes=64)
            for h in range(PATCHES):
                side = "left" if h == 0 else "right" if h == PATCHES - 1 else "mid"
                xk = patch_tiles[(e, h)]
                sums = to_scalar.tile([P, PACK, P], F32, name="sums", tag="s")
                nodes = STRIP * WINDOWS[h]
                for t in range(PACK):
                    nc.tensor.matmul(
                        out=sums[:, t, 0:nodes].rearrange("p (y x) -> p y x", x=WINDOWS[h]),
                        lhsT=xk[:, t:F_IN:PACK],
                        rhs=neighbours[(level, side)][:].rearrange("p (y x) -> p y x", x=WIDEST)[
                            :, :, 0 : WINDOWS[h]
                        ],
                        start=True,
                        stop=True,
                    )
                col = WINDOW_COL[h]
                nc.scalar.copy(
                    out=ax[:, :, col : col + WINDOWS[h], :],
                    in_=sums[:, :, 0:nodes].rearrange("p t (y x) -> p y x t", x=WINDOWS[h]),
                )
            strip_ax[e] = ax

        def quantise_strip(e):
            codes = work.tile([P, STRIP_NODES], U32, name="strip_codes", align_bytes=64)
            scales = work.tile([P, STRIP_NODES], U8, name="strip_scales", align_bytes=64)
            flat = strip_ax[e][:].rearrange("p r c t -> p (r c t)")
            for lo, hi in ((0, 2 * P), (2 * P, 3 * P)):
                nc.vector.quantize_mx(
                    out=codes[:, lo:hi].bitcast(FP8X4),
                    scales=scales[:, lo:hi],
                    in_=flat[:, lo * PACK : hi * PACK],
                )
            strip_mx[e] = (codes, scales)

        ctx.enter_context(tc.manual_schedule())

        transpose_unit("band", 0)
        transpose_unit("band", 1)
        transpose_unit("band", 2)
        sum_strip(0)
        first_add(0)
        first_add(1)
        second_add(0)
        transpose_unit("band", 3)
        transpose_bias()
        spread_bias()
        turned = BANDS - DIRECT_BANDS
        for g in range(BANDS):
            strip_node = (STRIP_TOP + g * STRIP) * GRID
            if g + BANDS_AHEAD + 1 < BANDS:
                load_unit("band", g + BANDS_AHEAD + 1)
            if g + STRIPS_AHEAD + 1 < STRIPS:
                load_strip(g + STRIPS_AHEAD + 1)
            if g < STRIPS:
                quantise_strip(g)
                products = [multiply_direct(*strip_mx[g], q) for q in range(STRIP_TILES - 1)]
            quantise(g)
            if g + 2 < BANDS:
                first_add(g + 2)
            if g < turned:
                multiply(g)
            if g < STRIPS:
                add_bias(products[0], strip_node)
                products.append(multiply_direct(*strip_mx[g], STRIP_TILES - 1))
                add_bias(products[1], strip_node + P)
            if g == 0:
                sum_strip(1)
                transpose_unit("edge", 0)
                transpose_unit("edge", 1)
            if g + STRIPS_AHEAD < STRIPS:
                sum_strip(g + STRIPS_AHEAD)
            if 0 <= g - 1 < turned:
                transpose_back(g - 1)
            if g + 1 < BANDS:
                second_add(g + 1)
            if g + BANDS_AHEAD < BANDS:
                transpose_unit("band", g + BANDS_AHEAD)
            if g < STRIPS:
                add_bias(products[2], strip_node + 2 * P)
            if g >= turned:
                for q in range(TILES):
                    add_bias(multiply_direct(*mx_tiles[g], q), place(g)[2] * GRID + q * P)
